import numpy as np
import ml_dtypes


def mxq(x, axis, fmt="e4m3"):
    dtype, down = {"e4m3": (ml_dtypes.float8_e4m3fn, 7), "e5m2": (ml_dtypes.float8_e5m2, 14)}[fmt]
    v = np.moveaxis(np.asarray(x, np.float32).astype(ml_dtypes.bfloat16).astype(np.float64), axis, -1)
    blocks = v.reshape(v.shape[:-1] + (-1, 32))
    amax = np.abs(blocks).max(-1, keepdims=True)
    byte = np.maximum(np.where(amax > 0, np.frexp(amax)[1] - 1 + 127, 0) - down, 1)
    scale = np.exp2(byte - 127.0)
    codes = (blocks / scale).astype(np.float32).astype(dtype).astype(np.float64)
    return np.moveaxis((codes * scale).reshape(v.shape), -1, axis)


WIDE = False


def mx_kscale(k):
    if not WIDE:
        return np.ones(k)
    levels = np.array([10, -10, 5, -5, 0])
    if k % 512:
        return np.exp2(np.random.permutation(np.resize(levels, k // 32))).repeat(32)
    a = np.empty((k // 512, 16))
    for p in range(k // 512):
        a[p, :8] = np.random.permutation(np.resize(levels, 8))
        for g in range(8):
            far = levels[np.abs(levels - a[p, g]) >= 10]
            a[p, g + 8] = far[np.random.randint(len(far))]
    return np.exp2(a.ravel()).repeat(32)


BF16 = ml_dtypes.bfloat16


def bf(x):
    return np.asarray(x, np.float32).astype(BF16)


def f64(x):
    return np.asarray(x).astype(np.float64)


B, T, HP, WP, NH, D, DFF = 16, 8, 6, 6, 16, 512, 4096
HW = HP * WP


def setup_inputs():
    s = mx_kscale(D)
    c = np.random.standard_normal((B * T, 1 + HW, D)) * 1.5 / np.sqrt(1 + HW)
    c[:, 0, :] *= 5.0
    return {"ctx_s": bf(c * s),
            "x_res": bf(np.random.standard_normal((B, 1 + HW * T, D)) * 1.1),
            "s_out_w": bf(np.random.standard_normal((D, D)) / np.sqrt(D) / s[:, None]),
            "s_out_b": bf(0.1 * np.random.standard_normal(D))}


def reference(ctx_s, x_res, s_out_w, s_out_b):
    res_s = (mxq(f64(ctx_s), 2, "e4m3") @ mxq(f64(s_out_w), 0, "e4m3")) + f64(s_out_b)
    cls_tok = res_s[:, 0, :].reshape(B, T, D).mean(axis=1, keepdims=True)
    res_p = res_s[:, 1:, :].reshape(B, T, HW, D).swapaxes(1, 2).reshape(B, HW * T, D)
    return f64(x_res) + np.concatenate([cls_tok, res_p], axis=1)

@@ -1,0 +1,283 @@
+from contextlib import ExitStack
+
+import concourse.mybir as mybir
+from concourse.masks import make_identity
+
+F32 = mybir.dt.float32
+BF16 = mybir.dt.bfloat16
+U32 = mybir.dt.uint32
+U8 = mybir.dt.uint8
+FP8X4 = mybir.dt.float8_e4m3fn_x4
+ADD = mybir.AluOpType.add
+IDENTITY = mybir.ActivationFunctionType.Identity
+
+P = 128
+PACK = 4
+SAMPLES = 16
+FRAMES = 8
+PATCHES = 36
+D = 512
+D_TILES = D // P
+
+CHUNK_PATCHES = 4
+CHUNKS = PATCHES // CHUNK_PATCHES
+GROUP_TILES = 4
+GROUP_TOKENS = GROUP_TILES * P
+
+MAIN_RUN = 2
+MAIN_ROWS = P * MAIN_RUN
+MAIN_CHUNKS = MAIN_ROWS // FRAMES // CHUNK_PATCHES
+GROUP_SAMPLES = GROUP_TILES // MAIN_RUN
+MAIN_GROUPS = SAMPLES // GROUP_SAMPLES
+TAIL_RUN = 4
+TAIL = MAIN_GROUPS
+TURN = 4
+
+FLOPS = 2 * SAMPLES * FRAMES * (1 + PATCHES) * D * D
+
+
+def transpose_words(nc, flipped, rows, permutation):
+    words = rows.bitcast(F32)
+    for u in range(2):
+        nc.tensor.transpose(flipped[:, u, :], words[:, u::2], permutation)
+
+
+def rows_in_hbm(tensor, g):
+    if g == TAIL:
+        return tensor[:, 1 + MAIN_ROWS :, :].rearrange("b (x j) d -> b x (j d)", j=TAIL_RUN)
+    samples = tensor[g * GROUP_SAMPLES : (g + 1) * GROUP_SAMPLES, 1 : 1 + MAIN_ROWS, :]
+    return samples.rearrange("s (p j) d -> p s (j d)", j=MAIN_RUN)
+
+
+def rows_in_sbuf(tiles, g):
+    if g == TAIL:
+        return tiles[:].rearrange("p j d -> p (j d)")
+    return tiles[:].rearrange("p (s j) d -> p s (j d)", j=MAIN_RUN)
+
+
+def tile_timesformerlayer_pc_t_kernel(tc, ctx_s, x_res, s_out_w, s_out_b, out):
+    nc = tc.nc
+    with ExitStack() as scope:
+        const = scope.enter_context(tc.tile_pool(name="const", bufs=1))
+        resident = scope.enter_context(tc.tile_pool(name="resident", bufs=1))
+        work = scope.enter_context(tc.tile_pool(name="work", bufs=3))
+        stores = scope.enter_context(tc.tile_pool(name="stores", bufs=4))
+        psum = scope.enter_context(tc.psum_pool(name="psum", bufs=8))
+        scope.enter_context(tc.manual_schedule())
+
+        group_order = [TAIL] + list(range(MAIN_GROUPS))
+
+        bias_rows = const.tile([P, P], BF16)
+        nc.vector.memset(bias_rows[:], 0.0)
+        nc.sync.dma_start(
+            out=bias_rows[0:D_TILES, :], in_=s_out_b.rearrange("(m d) -> m d", m=D_TILES)
+        )
+        w_rows = const.tile([P, PACK, D], BF16)
+        nc.sync.dma_start(out=w_rows[:], in_=s_out_w.rearrange("(q v) c -> q v c", v=PACK))
+        cls_ctx = resident.tile([P, D], BF16)
+        nc.sync.dma_start(out=cls_ctx[:], in_=ctx_s[:, 0, :])
+        cls_x = resident.tile([SAMPLES, D], BF16)
+        nc.sync.dma_start(out=cls_x[:], in_=x_res[:, 0, :])
+        ctx_chunks = {}
+        for c in group_order:
+            ctx_chunk = resident.tile([P, CHUNK_PATCHES, D], BF16, name="ctx_chunk%d" % c)
+            first = 1 + c * CHUNK_PATCHES
+            nc.sync.dma_start(out=ctx_chunk[:], in_=ctx_s[:, first : first + CHUNK_PATCHES, :])
+            ctx_chunks[c] = ctx_chunk
+        x_groups = {}
+        for g in group_order:
+            x_group = resident.tile([P, GROUP_TILES, D], BF16, name="x_group%d" % g)
+            nc.sync.dma_start(out=rows_in_sbuf(x_group, g), in_=rows_in_hbm(x_res, g))
+            x_groups[g] = x_group
+
+        ident = const.tile([P, P], F32)
+        make_identity(nc, ident[:])
+        ident_bf16 = const.tile([P, P], BF16)
+        nc.vector.tensor_copy(out=ident_bf16[:], in_=ident[:])
+        main_order = const.tile([P, P], F32)
+        nc.vector.tensor_copy(
+            out=main_order[:].rearrange("n (b j h) -> n b j h", j=MAIN_RUN, h=FRAMES // MAIN_RUN),
+            in_=ident[:].rearrange("n (b h j) -> n b j h", j=MAIN_RUN, h=FRAMES // MAIN_RUN),
+        )
+        tail_order = const.tile([P, P], F32)
+        nc.vector.tensor_copy(
+            out=tail_order[:].rearrange("n (j g) -> n j g", j=TAIL_RUN),
+            in_=ident[:].rearrange("n (g j) -> n j g", j=TAIL_RUN),
+        )
+        bias_flipped = psum.tile([P, P], BF16, tag="bank")
+        nc.tensor.transpose(bias_flipped[:], bias_rows[:], ident_bf16[:])
+        bias_col = const.tile([P, D_TILES], F32)
+        nc.scalar.copy(out=bias_col[:], in_=bias_flipped[:, 0:D_TILES])
+
+        w_grouped = const.tile([P, D, PACK], BF16, align_bytes=64)
+        nc.vector.tensor_copy(out=w_grouped[:], in_=w_rows[:].rearrange("q v c -> q c v"))
+        w_codes = const.tile([P, D], U32, align_bytes=64)
+        w_scales = const.tile([P, D], U8, align_bytes=64)
+        nc.vector.quantize_mx(
+            out=w_codes[:].bitcast(FP8X4),
+            scales=w_scales[:],
+            in_=w_grouped[:].rearrange("q c v -> q (c v)"),
+        )
+
+        def multiply_by_w(prod, m, codes, scales):
+            columns = slice(m * P, (m + 1) * P)
+            nc.tensor.matmul_mx(
+                out=prod,
+                lhsT=w_codes[:, columns].bitcast(FP8X4),
+                lhsT_scale=w_scales[:, columns],
+                rhs=codes.bitcast(FP8X4),
+                rhs_scale=scales,
+                start=True,
+                stop=True,
+            )
+
+        cls_codes = const.tile([P, P], U32, align_bytes=64)
+        cls_scales = const.tile([P, P], U8, align_bytes=64)
+        cls_mean = const.tile([P, D_TILES, P], F32)
+        nc.vector.memset(cls_mean[:], 0.0)
+
+        def flip_class():
+            cls_flipped = psum.tile([P, 2, P], F32, tag="bank")
+            transpose_words(nc, cls_flipped, cls_ctx[:], ident[:])
+            cls_grouped = const.tile([P, P, PACK], BF16, align_bytes=64)
+            nc.scalar.copy(
+                out=cls_grouped[:].bitcast(F32), in_=cls_flipped[:].rearrange("q u n -> q n u")
+            )
+            nc.vector.quantize_mx(
+                out=cls_codes[:].bitcast(FP8X4),
+                scales=cls_scales[:],
+                in_=cls_grouped[:].rearrange("q n v -> q (n v)"),
+            )
+
+        def multiply_class():
+            cls_prod = psum.tile([P, D_TILES, P], F32, tag="bank")
+            for m in range(D_TILES):
+                multiply_by_w(cls_prod[:, m, :], m, cls_codes[:], cls_scales[:])
+            cls_sum = const.tile([P, D_TILES, SAMPLES], F32)
+            nc.vector.tensor_reduce(
+                out=cls_sum[:],
+                in_=cls_prod[:].rearrange("i m (b t) -> i m b t", t=FRAMES),
+                axis=mybir.AxisListType.X,
+                op=ADD,
+            )
+            for m in range(D_TILES):
+                nc.scalar.activation(
+                    out=cls_mean[:, m, 0:SAMPLES],
+                    in_=cls_sum[:, m, :],
+                    func=IDENTITY,
+                    bias=bias_col[:, m : m + 1],
+                    scale=1.0 / FRAMES,
+                )
+
+        def finish_class():
+            cls_back = psum.tile([P, D], F32, tag="bank")
+            for m in range(D_TILES):
+                nc.tensor.transpose(cls_back[:, m * P : (m + 1) * P], cls_mean[:, m, :], ident[:])
+            cls_out = const.tile([SAMPLES, D], F32)
+            nc.vector.tensor_tensor(
+                out=cls_out[:], in0=cls_back[0:SAMPLES, :], in1=cls_x[:], op=ADD
+            )
+            nc.sync.dma_start(out=out[:, 0, :], in_=cls_out[:])
+
+        main_tokens = resident.tile([P, SAMPLES * MAIN_RUN, P, PACK], BF16, align_bytes=64)
+        main_words = main_tokens[:].bitcast(F32)
+        tail_tokens = resident.tile(
+            [P, TAIL_RUN * SAMPLES, CHUNK_PATCHES, FRAMES // TAIL_RUN, PACK], BF16, align_bytes=64
+        )
+        tail_words = tail_tokens[:].bitcast(F32)
+
+        def flip(c):
+            for half in range(2):
+                flipped = psum.tile([P, 2, 2, P], F32, tag="bank")
+                for i in range(2):
+                    a = 2 * half + i
+                    order = tail_order if c == TAIL else main_order
+                    transpose_words(nc, flipped[:, i], ctx_chunks[c][:, a, :], order[:])
+                for i in range(2):
+                    a = 2 * half + i
+                    if c == TAIL:
+                        sorted_tokens = flipped[:, i].rearrange("q u (r h) -> q r h u", h=2)
+                        place = tail_words[:, :, a, :, :]
+                    else:
+                        sorted_tokens = flipped[:, i].rearrange("q u (r h) -> q r h u", h=4)
+                        first = 4 * (c * CHUNK_PATCHES + a)
+                        place = main_words[:, :, first : first + 4, :]
+                    if half == 0:
+                        nc.scalar.copy(out=place, in_=sorted_tokens)
+                    else:
+                        nc.vector.tensor_copy(out=place, in_=sorted_tokens)
+
+        quantised = {}
+        biased = {}
+        finished = {}
+
+        def quantise(g):
+            if g == TAIL:
+                tokens = tail_tokens[:].rearrange("q r a h v -> q (r a h v)")
+            else:
+                tiles = main_tokens[:, g * GROUP_TILES : (g + 1) * GROUP_TILES, :, :]
+                tokens = tiles.rearrange("q r p v -> q (r p v)")
+            codes = work.tile([P, GROUP_TOKENS], U32, align_bytes=64)
+            scales = work.tile([P, GROUP_TOKENS], U8, align_bytes=64)
+            nc.vector.quantize_mx(out=codes[:].bitcast(FP8X4), scales=scales[:], in_=tokens)
+            quantised[g] = (codes, scales)
+            biased[g] = work.tile([P, D_TILES, GROUP_TOKENS], F32, name="with_bias")
+            finished[g] = stores.tile([P, GROUP_TILES, D], F32, name="out_group")
+
+        def multiply(g, m):
+            codes, scales = quantised[g]
+            prod = psum.tile([P, GROUP_TOKENS], F32, tag="bank")
+            multiply_by_w(prod[:], m, codes[:], scales[:])
+            nc.scalar.activation(
+                out=biased[g][:, m, :],
+                in_=prod[:],
+                func=IDENTITY,
+                bias=bias_col[:, m : m + 1],
+                scale=1.0,
+            )
+
+        def finish(g, i):
+            back = psum.tile([P, D], F32, tag="bank")
+            for m in range(D_TILES):
+                nc.tensor.transpose(
+                    back[:, m * P : (m + 1) * P], biased[g][:, m, i * P : (i + 1) * P], ident[:]
+                )
+            nc.vector.tensor_tensor(
+                out=finished[g][:, i, :], in0=back[:], in1=x_groups[g][:, i, :], op=ADD
+            )
+
+        def store(g):
+            if g == TAIL:
+                nc.sync.dma_start(out=rows_in_hbm(out, g), in_=rows_in_sbuf(finished[g], g))
+            else:
+                for s in range(GROUP_SAMPLES):
+                    nc.sync.dma_start(
+                        out=rows_in_hbm(out, g)[:, s, :], in_=rows_in_sbuf(finished[g], g)[:, s, :]
+                    )
+
+        flip_class()
+        flip(TAIL)
+        quantise(TAIL)
+        flip(0)
+        multiply_class()
+        flip(1)
+        for m in range(D_TILES):
+            multiply(TAIL, m)
+        flip(2)
+        finish_class()
+        for c in range(3, MAIN_CHUNKS):
+            flip(c)
+        quantise(group_order[1])
+        for k in range(1, len(group_order)):
+            if k + 1 < len(group_order):
+                quantise(group_order[k + 1])
+            for first in range(0, GROUP_TILES, TURN):
+                for i in range(first, first + TURN):
+                    multiply(group_order[k], i)
+                for i in range(first, first + TURN):
+                    finish(group_order[k - 1], i)
+            store(group_order[k - 1])
+        last = group_order[len(group_order) - 1]
+        for i in range(GROUP_TILES):
+            finish(last, i)
+        store(last)

@@ -19,40 +19,32 @@ PATCHES = 36
 D = 512
 D_TILES = D // P
 
-CHUNK_PATCHES = 4
-CHUNKS = PATCHES // CHUNK_PATCHES
-GROUP_TILES = 4
-GROUP_TOKENS = GROUP_TILES * P
-
-MAIN_RUN = 2
-MAIN_ROWS = P * MAIN_RUN
-MAIN_CHUNKS = MAIN_ROWS // FRAMES // CHUNK_PATCHES
-GROUP_SAMPLES = GROUP_TILES // MAIN_RUN
-MAIN_GROUPS = SAMPLES // GROUP_SAMPLES
-TAIL_RUN = 4
-TAIL = MAIN_GROUPS
-TURN = 4
+LOAD_PATCHES = 4
+LOADS = PATCHES // LOAD_PATCHES
+SAMPLE_ROWS = 1 + FRAMES * PATCHES
+ROWS = SAMPLES * SAMPLE_ROWS
+RUN = 4
+CHUNK = RUN * P
+CHUNKS = ROWS // CHUNK
+REST = ROWS - CHUNKS * CHUNK
+TOKENS = ROWS + SAMPLE_ROWS
 
 FLOPS = 2 * SAMPLES * FRAMES * (1 + PATCHES) * D * D
 
 
-def transpose_words(nc, flipped, rows, permutation):
+def transpose_words(nc, flipped, rows, identity):
     words = rows.bitcast(F32)
     for u in range(2):
-        nc.tensor.transpose(flipped[:, u, :], words[:, u::2], permutation)
+        nc.tensor.transpose(flipped[:, u, :], words[:, u::2], identity)
 
 
-def rows_in_hbm(tensor, g):
-    if g == TAIL:
-        return tensor[:, 1 + MAIN_ROWS :, :].rearrange("b (x j) d -> b x (j d)", j=TAIL_RUN)
-    samples = tensor[g * GROUP_SAMPLES : (g + 1) * GROUP_SAMPLES, 1 : 1 + MAIN_ROWS, :]
-    return samples.rearrange("s (p j) d -> p s (j d)", j=MAIN_RUN)
+def chunk_rows(tensor, c):
+    rows = tensor.rearrange("b r d -> (b r) d")[c * CHUNK : (c + 1) * CHUNK, :]
+    return rows.rearrange("(p j) d -> p (j d)", j=RUN)
 
 
-def rows_in_sbuf(tiles, g):
-    if g == TAIL:
-        return tiles[:].rearrange("p j d -> p (j d)")
-    return tiles[:].rearrange("p (s j) d -> p s (j d)", j=MAIN_RUN)
+def rest_rows(tensor):
+    return tensor[SAMPLES - 1, SAMPLE_ROWS - REST :, :]
 
 
 def tile_timesformerlayer_pc_t_kernel(tc, ctx_s, x_res, s_out_w, s_out_b, out):
@@ -61,63 +53,66 @@ def tile_timesformerlayer_pc_t_kernel(tc, ctx_s, x_res, s_out_w, s_out_b, out):
         const = scope.enter_context(tc.tile_pool(name="const", bufs=1))
         resident = scope.enter_context(tc.tile_pool(name="resident", bufs=1))
         work = scope.enter_context(tc.tile_pool(name="work", bufs=3))
-        stores = scope.enter_context(tc.tile_pool(name="stores", bufs=4))
+        stores = scope.enter_context(tc.tile_pool(name="stores", bufs=6))
         psum = scope.enter_context(tc.psum_pool(name="psum", bufs=8))
         scope.enter_context(tc.manual_schedule())
 
-        group_order = [TAIL] + list(range(MAIN_GROUPS))
-
         bias_rows = const.tile([P, P], BF16)
         nc.vector.memset(bias_rows[:], 0.0)
+        first_ctx = resident.tile([P, 1 + LOAD_PATCHES, D], BF16)
+        nc.sync.dma_start(out=first_ctx[:], in_=ctx_s[:, 0 : 1 + LOAD_PATCHES, :])
         nc.sync.dma_start(
             out=bias_rows[0:D_TILES, :], in_=s_out_b.rearrange("(m d) -> m d", m=D_TILES)
         )
         w_rows = const.tile([P, PACK, D], BF16)
         nc.sync.dma_start(out=w_rows[:], in_=s_out_w.rearrange("(q v) c -> q v c", v=PACK))
-        cls_ctx = resident.tile([P, D], BF16)
-        nc.sync.dma_start(out=cls_ctx[:], in_=ctx_s[:, 0, :])
-        cls_x = resident.tile([SAMPLES, D], BF16)
-        nc.sync.dma_start(out=cls_x[:], in_=x_res[:, 0, :])
-        ctx_chunks = {}
-        for c in group_order:
-            ctx_chunk = resident.tile([P, CHUNK_PATCHES, D], BF16, name="ctx_chunk%d" % c)
-            first = 1 + c * CHUNK_PATCHES
-            nc.sync.dma_start(out=ctx_chunk[:], in_=ctx_s[:, first : first + CHUNK_PATCHES, :])
-            ctx_chunks[c] = ctx_chunk
-        x_groups = {}
-        for g in group_order:
-            x_group = resident.tile([P, GROUP_TILES, D], BF16, name="x_group%d" % g)
-            nc.sync.dma_start(out=rows_in_sbuf(x_group, g), in_=rows_in_hbm(x_res, g))
-            x_groups[g] = x_group
+        ctx_loads = [first_ctx[:, 1:, :]]
+        for c in range(1, LOADS):
+            ctx_load = resident.tile([P, LOAD_PATCHES, D], BF16, name="ctx%d" % c)
+            first = 1 + c * LOAD_PATCHES
+            nc.sync.dma_start(out=ctx_load[:], in_=ctx_s[:, first : first + LOAD_PATCHES, :])
+            ctx_loads.append(ctx_load[:])
+        x_chunks = []
+        for c in range(CHUNKS):
+            x_chunk = resident.tile([P, RUN, D], BF16, name="x%d" % c)
+            nc.sync.dma_start(
+                out=x_chunk[:].rearrange("p j d -> p (j d)"), in_=chunk_rows(x_res, c)
+            )
+            x_chunks.append(x_chunk)
+        rest_x = resident.tile([REST, D], BF16)
+        nc.sync.dma_start(out=rest_x[:], in_=rest_rows(x_res))
 
+        tokens = resident.tile([P, TOKENS, PACK], BF16, align_bytes=64)
+        token_words = tokens[:].bitcast(F32)
+        samples = tokens[:, 0:ROWS, :].rearrange("q (b r) v -> q b r v", r=SAMPLE_ROWS)
+        nc.vector.memset(samples[:, :, 0, :], 0.0)
+        nc.vector.memset(tokens[:, ROWS : CHUNKS * CHUNK + P, :], 0.0)
         ident = const.tile([P, P], F32)
         make_identity(nc, ident[:])
         ident_bf16 = const.tile([P, P], BF16)
         nc.vector.tensor_copy(out=ident_bf16[:], in_=ident[:])
-        main_order = const.tile([P, P], F32)
-        nc.vector.tensor_copy(
-            out=main_order[:].rearrange("n (b j h) -> n b j h", j=MAIN_RUN, h=FRAMES // MAIN_RUN),
-            in_=ident[:].rearrange("n (b h j) -> n b j h", j=MAIN_RUN, h=FRAMES // MAIN_RUN),
-        )
-        tail_order = const.tile([P, P], F32)
-        nc.vector.tensor_copy(
-            out=tail_order[:].rearrange("n (j g) -> n j g", j=TAIL_RUN),
-            in_=ident[:].rearrange("n (g j) -> n j g", j=TAIL_RUN),
-        )
-        bias_flipped = psum.tile([P, P], BF16, tag="bank")
-        nc.tensor.transpose(bias_flipped[:], bias_rows[:], ident_bf16[:])
-        bias_col = const.tile([P, D_TILES], F32)
-        nc.scalar.copy(out=bias_col[:], in_=bias_flipped[:, 0:D_TILES])
+        rest_biased = const.tile([P, D_TILES, P], F32)
+        nc.vector.memset(rest_biased[:], 0.0)
 
+        bias_col = const.tile([P, D_TILES], F32)
         w_grouped = const.tile([P, D, PACK], BF16, align_bytes=64)
-        nc.vector.tensor_copy(out=w_grouped[:], in_=w_rows[:].rearrange("q v c -> q c v"))
         w_codes = const.tile([P, D], U32, align_bytes=64)
         w_scales = const.tile([P, D], U8, align_bytes=64)
-        nc.vector.quantize_mx(
-            out=w_codes[:].bitcast(FP8X4),
-            scales=w_scales[:],
-            in_=w_grouped[:].rearrange("q c v -> q (c v)"),
-        )
+
+        def prepare_bias():
+            bias_flipped = psum.tile([P, P], BF16, tag="bank")
+            nc.tensor.transpose(bias_flipped[:], bias_rows[:], ident_bf16[:])
+            nc.scalar.copy(out=bias_col[:], in_=bias_flipped[:, 0:D_TILES])
+
+        def group_w():
+            nc.vector.tensor_copy(out=w_grouped[:], in_=w_rows[:].rearrange("q v c -> q c v"))
+
+        def quantise_w():
+            nc.vector.quantize_mx(
+                out=w_codes[:].bitcast(FP8X4),
+                scales=w_scales[:],
+                in_=w_grouped[:].rearrange("q c v -> q (c v)"),
+            )
 
         def multiply_by_w(prod, m, codes, scales):
             columns = slice(m * P, (m + 1) * P)
@@ -131,28 +126,33 @@ def tile_timesformerlayer_pc_t_kernel(tc, ctx_s, x_res, s_out_w, s_out_b, out):
                 stop=True,
             )
 
+        cls_grouped = const.tile([P, P, PACK], BF16, align_bytes=64)
         cls_codes = const.tile([P, P], U32, align_bytes=64)
         cls_scales = const.tile([P, P], U8, align_bytes=64)
-        cls_mean = const.tile([P, D_TILES, P], F32)
-        nc.vector.memset(cls_mean[:], 0.0)
+        cls_mean = const.tile([P, D_TILES, SAMPLES], F32)
 
         def flip_class():
             cls_flipped = psum.tile([P, 2, P], F32, tag="bank")
-            transpose_words(nc, cls_flipped, cls_ctx[:], ident[:])
-            cls_grouped = const.tile([P, P, PACK], BF16, align_bytes=64)
+            transpose_words(nc, cls_flipped, first_ctx[:, 0, :], ident[:])
             nc.scalar.copy(
                 out=cls_grouped[:].bitcast(F32), in_=cls_flipped[:].rearrange("q u n -> q n u")
             )
+
+        def quantise_class():
             nc.vector.quantize_mx(
                 out=cls_codes[:].bitcast(FP8X4),
                 scales=cls_scales[:],
                 in_=cls_grouped[:].rearrange("q n v -> q (n v)"),
             )
 
-        def multiply_class():
-            cls_prod = psum.tile([P, D_TILES, P], F32, tag="bank")
+        def multiply_128(codes, scales):
+            prod = psum.tile([P, D_TILES, P], F32, tag="bank")
             for m in range(D_TILES):
-                multiply_by_w(cls_prod[:, m, :], m, cls_codes[:], cls_scales[:])
+                multiply_by_w(prod[:, m, :], m, codes, scales)
+            return prod
+
+        def multiply_class():
+            cls_prod = multiply_128(cls_codes[:], cls_scales[:])
             cls_sum = const.tile([P, D_TILES, SAMPLES], F32)
             nc.vector.tensor_reduce(
                 out=cls_sum[:],
@@ -162,46 +162,26 @@ def tile_timesformerlayer_pc_t_kernel(tc, ctx_s, x_res, s_out_w, s_out_b, out):
             )
             for m in range(D_TILES):
                 nc.scalar.activation(
-                    out=cls_mean[:, m, 0:SAMPLES],
+                    out=cls_mean[:, m, :],
                     in_=cls_sum[:, m, :],
                     func=IDENTITY,
                     bias=bias_col[:, m : m + 1],
                     scale=1.0 / FRAMES,
                 )
 
-        def finish_class():
-            cls_back = psum.tile([P, D], F32, tag="bank")
-            for m in range(D_TILES):
-                nc.tensor.transpose(cls_back[:, m * P : (m + 1) * P], cls_mean[:, m, :], ident[:])
-            cls_out = const.tile([SAMPLES, D], F32)
-            nc.vector.tensor_tensor(
-                out=cls_out[:], in0=cls_back[0:SAMPLES, :], in1=cls_x[:], op=ADD
-            )
-            nc.sync.dma_start(out=out[:, 0, :], in_=cls_out[:])
-
-        main_tokens = resident.tile([P, SAMPLES * MAIN_RUN, P, PACK], BF16, align_bytes=64)
-        main_words = main_tokens[:].bitcast(F32)
-        tail_tokens = resident.tile(
-            [P, TAIL_RUN * SAMPLES, CHUNK_PATCHES, FRAMES // TAIL_RUN, PACK], BF16, align_bytes=64
-        )
-        tail_words = tail_tokens[:].bitcast(F32)
-
         def flip(c):
             for half in range(2):
                 flipped = psum.tile([P, 2, 2, P], F32, tag="bank")
                 for i in range(2):
-                    a = 2 * half + i
-                    order = tail_order if c == TAIL else main_order
-                    transpose_words(nc, flipped[:, i], ctx_chunks[c][:, a, :], order[:])
+                    transpose_words(
+                        nc, flipped[:, i], ctx_loads[c][:, 2 * half + i, :], ident[:]
+                    )
                 for i in range(2):
-                    a = 2 * half + i
-                    if c == TAIL:
-                        sorted_tokens = flipped[:, i].rearrange("q u (r h) -> q r h u", h=2)
-                        place = tail_words[:, :, a, :, :]
-                    else:
-                        sorted_tokens = flipped[:, i].rearrange("q u (r h) -> q r h u", h=4)
-                        first = 4 * (c * CHUNK_PATCHES + a)
-                        place = main_words[:, :, first : first + 4, :]
+                    first = 1 + FRAMES * (c * LOAD_PATCHES + 2 * half + i)
+                    place = token_words[:, first : first + ROWS, :].rearrange(
+                        "q (b r) u -> q b r u", r=SAMPLE_ROWS
+                    )[:, :, 0:FRAMES, :]
+                    sorted_tokens = flipped[:, i].rearrange("q u (b t) -> q b t u", t=FRAMES)
                     if half == 0:
                         nc.scalar.copy(out=place, in_=sorted_tokens)
                     else:
@@ -211,73 +191,112 @@ def tile_timesformerlayer_pc_t_kernel(tc, ctx_s, x_res, s_out_w, s_out_b, out):
         biased = {}
         finished = {}
 
-        def quantise(g):
-            if g == TAIL:
-                tokens = tail_tokens[:].rearrange("q r a h v -> q (r a h v)")
-            else:
-                tiles = main_tokens[:, g * GROUP_TILES : (g + 1) * GROUP_TILES, :, :]
-                tokens = tiles.rearrange("q r p v -> q (r p v)")
-            codes = work.tile([P, GROUP_TOKENS], U32, align_bytes=64)
-            scales = work.tile([P, GROUP_TOKENS], U8, align_bytes=64)
-            nc.vector.quantize_mx(out=codes[:].bitcast(FP8X4), scales=scales[:], in_=tokens)
-            quantised[g] = (codes, scales)
-            biased[g] = work.tile([P, D_TILES, GROUP_TOKENS], F32, name="with_bias")
-            finished[g] = stores.tile([P, GROUP_TILES, D], F32, name="out_group")
+        def quantise(c):
+            codes = work.tile([P, CHUNK], U32, align_bytes=64)
+            scales = work.tile([P, CHUNK], U8, align_bytes=64)
+            nc.vector.quantize_mx(
+                out=codes[:].bitcast(FP8X4),
+                scales=scales[:],
+                in_=tokens[:, c * CHUNK : (c + 1) * CHUNK, :].rearrange("q r v -> q (r v)"),
+            )
+            quantised[c] = (codes, scales)
+            biased[c] = work.tile([P, D_TILES, RUN, P], F32, name="with_bias")
+            finished[c] = stores.tile([P, RUN, D], F32, name="out_chunk")
 
-        def multiply(g, m):
-            codes, scales = quantised[g]
-            prod = psum.tile([P, GROUP_TOKENS], F32, tag="bank")
+        def multiply(c, m):
+            codes, scales = quantised[c]
+            prod = psum.tile([P, CHUNK], F32, tag="bank")
             multiply_by_w(prod[:], m, codes[:], scales[:])
             nc.scalar.activation(
-                out=biased[g][:, m, :],
-                in_=prod[:],
+                out=biased[c][:, m, :, :],
+                in_=prod[:].rearrange("i (p j) -> i j p", j=RUN),
                 func=IDENTITY,
                 bias=bias_col[:, m : m + 1],
                 scale=1.0,
             )
 
-        def finish(g, i):
+        def place_class(c):
+            for b in range(SAMPLES):
+                row = b * SAMPLE_ROWS - c * CHUNK
+                if 0 <= row < CHUNK:
+                    p, j = divmod(row, RUN)
+                    nc.scalar.copy(out=biased[c][:, :, j, p : p + 1], in_=cls_mean[:, :, b : b + 1])
+
+        def finish(c, j):
             back = psum.tile([P, D], F32, tag="bank")
             for m in range(D_TILES):
                 nc.tensor.transpose(
-                    back[:, m * P : (m + 1) * P], biased[g][:, m, i * P : (i + 1) * P], ident[:]
+                    back[:, m * P : (m + 1) * P], biased[c][:, m, j, :], ident[:]
                 )
             nc.vector.tensor_tensor(
-                out=finished[g][:, i, :], in0=back[:], in1=x_groups[g][:, i, :], op=ADD
+                out=finished[c][:, j, :], in0=back[:], in1=x_chunks[c][:, j, :], op=ADD
             )
 
-        def store(g):
-            if g == TAIL:
-                nc.sync.dma_start(out=rows_in_hbm(out, g), in_=rows_in_sbuf(finished[g], g))
-            else:
-                for s in range(GROUP_SAMPLES):
-                    nc.sync.dma_start(
-                        out=rows_in_hbm(out, g)[:, s, :], in_=rows_in_sbuf(finished[g], g)[:, s, :]
-                    )
+        def store(c):
+            nc.sync.dma_start(
+                out=chunk_rows(out, c), in_=finished[c][:].rearrange("p j d -> p (j d)")
+            )
+
+        rest_codes = const.tile([P, P], U32, align_bytes=64)
+        rest_scales = const.tile([P, P], U8, align_bytes=64)
+
+        def quantise_rest():
+            first = CHUNKS * CHUNK
+            nc.vector.quantize_mx(
+                out=rest_codes[:].bitcast(FP8X4),
+                scales=rest_scales[:],
+                in_=tokens[:, first : first + P, :].rearrange("q r v -> q (r v)"),
+            )
+
+        def multiply_rest():
+            rest_prod = multiply_128(rest_codes[:], rest_scales[:])
+            for m in range(D_TILES):
+                nc.scalar.activation(
+                    out=rest_biased[:, m, 0:REST],
+                    in_=rest_prod[:, m, 0:REST],
+                    func=IDENTITY,
+                    bias=bias_col[:, m : m + 1],
+                    scale=1.0,
+                )
+
+        def finish_rest():
+            rest_back = psum.tile([P, D], F32, tag="bank")
+            for m in range(D_TILES):
+                nc.tensor.transpose(
+                    rest_back[:, m * P : (m + 1) * P], rest_biased[:, m, :], ident[:]
+                )
+            rest_out = const.tile([REST, D], F32)
+            nc.vector.tensor_tensor(
+                out=rest_out[:], in0=rest_back[0:REST, :], in1=rest_x[:], op=ADD
+            )
+            nc.sync.dma_start(out=rest_rows(out), in_=rest_out[:])
 
         flip_class()
-        flip(TAIL)
-        quantise(TAIL)
+        prepare_bias()
         flip(0)
-        multiply_class()
+        group_w()
+        quantise_class()
         flip(1)
-        for m in range(D_TILES):
-            multiply(TAIL, m)
+        quantise_w()
         flip(2)
-        finish_class()
-        for c in range(3, MAIN_CHUNKS):
+        multiply_class()
+        for c in range(3, LOADS):
             flip(c)
-        quantise(group_order[1])
-        for k in range(1, len(group_order)):
-            if k + 1 < len(group_order):
-                quantise(group_order[k + 1])
-            for first in range(0, GROUP_TILES, TURN):
-                for i in range(first, first + TURN):
-                    multiply(group_order[k], i)
-                for i in range(first, first + TURN):
-                    finish(group_order[k - 1], i)
-            store(group_order[k - 1])
-        last = group_order[len(group_order) - 1]
-        for i in range(GROUP_TILES):
-            finish(last, i)
-        store(last)
+        quantise(0)
+        for c in range(CHUNKS):
+            if c + 1 < CHUNKS:
+                quantise(c + 1)
+            else:
+                quantise_rest()
+            for m in range(D_TILES):
+                multiply(c, m)
+            place_class(c)
+            if c > 0:
+                for j in range(RUN):
+                    finish(c - 1, j)
+                store(c - 1)
+        multiply_rest()
+        for j in range(RUN):
+            finish(CHUNKS - 1, j)
+        store(CHUNKS - 1)
+        finish_rest()

@@ -19,8 +19,14 @@ PATCHES = 36
 D = 512
 D_TILES = D // P
 
-LOAD_PATCHES = 4
-LOADS = PATCHES // LOAD_PATCHES
+HALF_SAMPLES = SAMPLES // 2
+PARTS = 2
+PART_PATCHES = PATCHES // PARTS
+LOAD_TILES = 6
+LOADS = PART_PATCHES // LOAD_TILES
+PAIRS = PART_PATCHES // 2
+FLIP_CHUNKS = 3
+FLIP_PAIRS = PAIRS // FLIP_CHUNKS
 SAMPLE_ROWS = 1 + FRAMES * PATCHES
 ROWS = SAMPLES * SAMPLE_ROWS
 RUN = 4
@@ -32,10 +38,10 @@ TOKENS = ROWS + SAMPLE_ROWS
 FLOPS = 2 * SAMPLES * FRAMES * (1 + PATCHES) * D * D
 
 
-def transpose_words(nc, flipped, rows, identity):
+def transpose_words(nc, flipped, rows, permutation):
     words = rows.bitcast(F32)
     for u in range(2):
-        nc.tensor.transpose(flipped[:, u, :], words[:, u::2], identity)
+        nc.tensor.transpose(flipped[:, u, :], words[:, u::2], permutation)
 
 
 def chunk_rows(tensor, c):
@@ -59,26 +65,43 @@ def tile_timesformerlayer_pc_t_kernel(tc, ctx_s, x_res, s_out_w, s_out_b, out):
 
         bias_rows = const.tile([P, P], BF16)
         nc.vector.memset(bias_rows[:], 0.0)
-        first_ctx = resident.tile([P, 1 + LOAD_PATCHES, D], BF16)
-        nc.sync.dma_start(out=first_ctx[:], in_=ctx_s[:, 0 : 1 + LOAD_PATCHES, :])
-        nc.sync.dma_start(
-            out=bias_rows[0:D_TILES, :], in_=s_out_b.rearrange("(m d) -> m d", m=D_TILES)
-        )
-        w_rows = const.tile([P, PACK, D], BF16)
-        nc.sync.dma_start(out=w_rows[:], in_=s_out_w.rearrange("(q v) c -> q v c", v=PACK))
-        ctx_loads = [first_ctx[:, 1:, :]]
-        for c in range(1, LOADS):
-            ctx_load = resident.tile([P, LOAD_PATCHES, D], BF16, name="ctx%d" % c)
-            first = 1 + c * LOAD_PATCHES
-            nc.sync.dma_start(out=ctx_load[:], in_=ctx_s[:, first : first + LOAD_PATCHES, :])
-            ctx_loads.append(ctx_load[:])
+        ctx_loads = []
         x_chunks = []
-        for c in range(CHUNKS):
+
+        def load_ctx(half, c):
+            ctx_load = resident.tile([P, LOAD_TILES, D], BF16, name="ctx%d%d" % (half, c))
+            sequences = ctx_s[half * P // PARTS : (half + 1) * P // PARTS, 1:, :]
+            patches = sequences.rearrange("s (i a) d -> s i a d", i=PARTS)
+            patches = patches[:, :, c * LOAD_TILES : (c + 1) * LOAD_TILES, :]
+            nc.sync.dma_start(
+                out=ctx_load[:].rearrange("n a d -> n (a d)"),
+                in_=patches.rearrange("s i a d -> s i (a d)"),
+            )
+            ctx_loads.append(ctx_load)
+
+        def load_x(c):
             x_chunk = resident.tile([P, RUN, D], BF16, name="x%d" % c)
             nc.sync.dma_start(
                 out=x_chunk[:].rearrange("p j d -> p (j d)"), in_=chunk_rows(x_res, c)
             )
             x_chunks.append(x_chunk)
+
+        load_ctx(0, 0)
+        nc.sync.dma_start(
+            out=bias_rows[0:D_TILES, :], in_=s_out_b.rearrange("(m d) -> m d", m=D_TILES)
+        )
+        w_rows = const.tile([P, PACK, D], BF16)
+        nc.sync.dma_start(out=w_rows[:], in_=s_out_w.rearrange("(q v) c -> q v c", v=PACK))
+        load_ctx(0, 1)
+        cls_ctx = resident.tile([P, D], BF16)
+        nc.sync.dma_start(out=cls_ctx[:], in_=ctx_s[:, 0, :])
+        load_ctx(0, 2)
+        load_ctx(1, 0)
+        load_x(0)
+        load_ctx(1, 1)
+        load_ctx(1, 2)
+        for c in range(1, CHUNKS):
+            load_x(c)
         rest_x = resident.tile([REST, D], BF16)
         nc.sync.dma_start(out=rest_x[:], in_=rest_rows(x_res))
 
@@ -89,6 +112,11 @@ def tile_timesformerlayer_pc_t_kernel(tc, ctx_s, x_res, s_out_w, s_out_b, out):
         nc.vector.memset(tokens[:, ROWS : CHUNKS * CHUNK + P, :], 0.0)
         ident = const.tile([P, P], F32)
         make_identity(nc, ident[:])
+        token_order = const.tile([P, P], F32)
+        nc.vector.tensor_copy(
+            out=token_order[:].rearrange("n (i s) -> n i s", i=PARTS),
+            in_=ident[:].rearrange("n (s i) -> n i s", i=PARTS),
+        )
         ident_bf16 = const.tile([P, P], BF16)
         nc.vector.tensor_copy(out=ident_bf16[:], in_=ident[:])
         rest_biased = const.tile([P, D_TILES, P], F32)
@@ -133,7 +161,7 @@ def tile_timesformerlayer_pc_t_kernel(tc, ctx_s, x_res, s_out_w, s_out_b, out):
 
         def flip_class():
             cls_flipped = psum.tile([P, 2, P], F32, tag="bank")
-            transpose_words(nc, cls_flipped, first_ctx[:, 0, :], ident[:])
+            transpose_words(nc, cls_flipped, cls_ctx[:], ident[:])
             nc.scalar.copy(
                 out=cls_grouped[:].bitcast(F32), in_=cls_flipped[:].rearrange("q u n -> q n u")
             )
@@ -169,23 +197,26 @@ def tile_timesformerlayer_pc_t_kernel(tc, ctx_s, x_res, s_out_w, s_out_b, out):
                     scale=1.0 / FRAMES,
                 )
 
-        def flip(c):
-            for half in range(2):
-                flipped = psum.tile([P, 2, 2, P], F32, tag="bank")
-                for i in range(2):
-                    transpose_words(
-                        nc, flipped[:, i], ctx_loads[c][:, 2 * half + i, :], ident[:]
-                    )
-                for i in range(2):
-                    first = 1 + FRAMES * (c * LOAD_PATCHES + 2 * half + i)
-                    place = token_words[:, first : first + ROWS, :].rearrange(
-                        "q (b r) u -> q b r u", r=SAMPLE_ROWS
-                    )[:, :, 0:FRAMES, :]
-                    sorted_tokens = flipped[:, i].rearrange("q u (b t) -> q b t u", t=FRAMES)
-                    if half == 0:
-                        nc.scalar.copy(out=place, in_=sorted_tokens)
-                    else:
-                        nc.vector.tensor_copy(out=place, in_=sorted_tokens)
+        def flip(half, pair):
+            c, first_tile = divmod(2 * pair, LOAD_TILES)
+            flipped = psum.tile([P, 2, 2 * P], F32, tag="bank")
+            by_tile = flipped[:].rearrange("q u (g k t) -> q k u g t", k=2, t=FRAMES)
+            for k in range(2):
+                rows = ctx_loads[half * LOADS + c][:, first_tile + k, :]
+                transpose_words(nc, by_tile[:, k], rows, token_order[:])
+            for i in range(PARTS):
+                patch = PART_PATCHES * i + 2 * pair
+                base = half * HALF_SAMPLES * SAMPLE_ROWS + 1 + FRAMES * patch
+                place = token_words[:, base : base + HALF_SAMPLES * SAMPLE_ROWS, :].rearrange(
+                    "q (b r) u -> q b r u", r=SAMPLE_ROWS
+                )[:, :, 0 : 2 * FRAMES, :]
+                sorted_tokens = flipped[:, :, i * P : (i + 1) * P].rearrange(
+                    "q u (b w) -> q b w u", w=2 * FRAMES
+                )
+                if pair % 2 == 0:
+                    nc.scalar.copy(out=place, in_=sorted_tokens)
+                else:
+                    nc.vector.tensor_copy(out=place, in_=sorted_tokens)
 
         quantised = {}
         biased = {}
@@ -271,29 +302,37 @@ def tile_timesformerlayer_pc_t_kernel(tc, ctx_s, x_res, s_out_w, s_out_b, out):
             )
             nc.sync.dma_start(out=rest_rows(out), in_=rest_out[:])
 
-        flip_class()
+        for pair in range(3):
+            flip(0, pair)
         prepare_bias()
-        flip(0)
         group_w()
-        quantise_class()
-        flip(1)
+        for pair in range(3, 6):
+            flip(0, pair)
         quantise_w()
-        flip(2)
-        multiply_class()
-        for c in range(3, LOADS):
-            flip(c)
+        flip_class()
+        for pair in range(6, PAIRS):
+            flip(0, pair)
+        quantise_class()
         quantise(0)
+        multiply_class()
+        pairs = list(range(PAIRS))
         for c in range(CHUNKS):
             if c + 1 < CHUNKS:
                 quantise(c + 1)
             else:
                 quantise_rest()
-            for m in range(D_TILES):
-                multiply(c, m)
-            place_class(c)
+            for half in range(2):
+                for m in range(2 * half, 2 * half + 2):
+                    multiply(c, m)
+                if half == 1:
+                    place_class(c)
+                if c > 0:
+                    for j in range(2 * half, 2 * half + 2):
+                        finish(c - 1, j)
+                if c < FLIP_CHUNKS:
+                    for pair in pairs[FLIP_PAIRS * c + 2 * half : FLIP_PAIRS * c + 2 + half]:
+                        flip(1, pair)
             if c > 0:
-                for j in range(RUN):
-                    finish(c - 1, j)
                 store(c - 1)
         multiply_rest()
         for j in range(RUN):

@@ -19,14 +19,12 @@ PATCHES = 36
 D = 512
 D_TILES = D // P
 
-HALF_SAMPLES = SAMPLES // 2
-PARTS = 2
-PART_PATCHES = PATCHES // PARTS
-LOAD_TILES = 6
-LOADS = PART_PATCHES // LOAD_TILES
-PAIRS = PART_PATCHES // 2
-FLIP_CHUNKS = 3
-FLIP_PAIRS = PAIRS // FLIP_CHUNKS
+QUARTERS = 4
+QUARTER_SAMPLES = SAMPLES // QUARTERS
+PARTS = 4
+TILES = PATCHES // PARTS
+PAIRS = (TILES + 1) // 2
+FIRST_TILES = 4
 SAMPLE_ROWS = 1 + FRAMES * PATCHES
 ROWS = SAMPLES * SAMPLE_ROWS
 RUN = 4
@@ -65,19 +63,19 @@ def tile_timesformerlayer_pc_t_kernel(tc, ctx_s, x_res, s_out_w, s_out_b, out):
 
         bias_rows = const.tile([P, P], BF16)
         nc.vector.memset(bias_rows[:], 0.0)
-        ctx_loads = []
+        ctx_tiles = {}
         x_chunks = []
 
-        def load_ctx(half, c):
-            ctx_load = resident.tile([P, LOAD_TILES, D], BF16, name="ctx%d%d" % (half, c))
-            sequences = ctx_s[half * P // PARTS : (half + 1) * P // PARTS, 1:, :]
+        def load_ctx(quarter, first, count):
+            ctx_load = resident.tile([P, count, D], BF16, name="ctx%d%d" % (quarter, first))
+            sequences = ctx_s[quarter * P // PARTS : (quarter + 1) * P // PARTS, 1:, :]
             patches = sequences.rearrange("s (i a) d -> s i a d", i=PARTS)
-            patches = patches[:, :, c * LOAD_TILES : (c + 1) * LOAD_TILES, :]
             nc.sync.dma_start(
                 out=ctx_load[:].rearrange("n a d -> n (a d)"),
-                in_=patches.rearrange("s i a d -> s i (a d)"),
+                in_=patches[:, :, first : first + count, :].rearrange("s i a d -> s i (a d)"),
             )
-            ctx_loads.append(ctx_load)
+            for a in range(count):
+                ctx_tiles[quarter, first + a] = ctx_load[:, a, :]
 
         def load_x(c):
             x_chunk = resident.tile([P, RUN, D], BF16, name="x%d" % c)
@@ -86,21 +84,19 @@ def tile_timesformerlayer_pc_t_kernel(tc, ctx_s, x_res, s_out_w, s_out_b, out):
             )
             x_chunks.append(x_chunk)
 
-        load_ctx(0, 0)
+        load_ctx(0, 0, FIRST_TILES)
         nc.sync.dma_start(
             out=bias_rows[0:D_TILES, :], in_=s_out_b.rearrange("(m d) -> m d", m=D_TILES)
         )
+        load_ctx(0, FIRST_TILES, TILES - FIRST_TILES)
         w_rows = const.tile([P, PACK, D], BF16)
         nc.sync.dma_start(out=w_rows[:], in_=s_out_w.rearrange("(q v) c -> q v c", v=PACK))
-        load_ctx(0, 1)
         cls_ctx = resident.tile([P, D], BF16)
         nc.sync.dma_start(out=cls_ctx[:], in_=ctx_s[:, 0, :])
-        load_ctx(0, 2)
-        load_ctx(1, 0)
-        load_x(0)
-        load_ctx(1, 1)
-        load_ctx(1, 2)
-        for c in range(1, CHUNKS):
+        for quarter in range(1, QUARTERS):
+            load_ctx(quarter, 0, TILES)
+            load_x(quarter - 1)
+        for c in range(QUARTERS - 1, CHUNKS):
             load_x(c)
         rest_x = resident.tile([REST, D], BF16)
         nc.sync.dma_start(out=rest_x[:], in_=rest_rows(x_res))
@@ -114,8 +110,8 @@ def tile_timesformerlayer_pc_t_kernel(tc, ctx_s, x_res, s_out_w, s_out_b, out):
         make_identity(nc, ident[:])
         token_order = const.tile([P, P], F32)
         nc.vector.tensor_copy(
-            out=token_order[:].rearrange("n (i s) -> n i s", i=PARTS),
-            in_=ident[:].rearrange("n (s i) -> n i s", i=PARTS),
+            out=token_order[:].rearrange("n (b i t) -> n b i t", i=PARTS, t=FRAMES),
+            in_=ident[:].rearrange("n (b t i) -> n b i t", i=PARTS, t=FRAMES),
         )
         ident_bf16 = const.tile([P, P], BF16)
         nc.vector.tensor_copy(out=ident_bf16[:], in_=ident[:])
@@ -197,26 +193,28 @@ def tile_timesformerlayer_pc_t_kernel(tc, ctx_s, x_res, s_out_w, s_out_b, out):
                     scale=1.0 / FRAMES,
                 )
 
-        def flip(half, pair):
-            c, first_tile = divmod(2 * pair, LOAD_TILES)
-            flipped = psum.tile([P, 2, 2 * P], F32, tag="bank")
-            by_tile = flipped[:].rearrange("q u (g k t) -> q k u g t", k=2, t=FRAMES)
-            for k in range(2):
-                rows = ctx_loads[half * LOADS + c][:, first_tile + k, :]
-                transpose_words(nc, by_tile[:, k], rows, token_order[:])
-            for i in range(PARTS):
-                patch = PART_PATCHES * i + 2 * pair
-                base = half * HALF_SAMPLES * SAMPLE_ROWS + 1 + FRAMES * patch
-                place = token_words[:, base : base + HALF_SAMPLES * SAMPLE_ROWS, :].rearrange(
-                    "q (b r) u -> q b r u", r=SAMPLE_ROWS
-                )[:, :, 0 : 2 * FRAMES, :]
-                sorted_tokens = flipped[:, :, i * P : (i + 1) * P].rearrange(
-                    "q u (b w) -> q b w u", w=2 * FRAMES
-                )
-                if pair % 2 == 0:
-                    nc.scalar.copy(out=place, in_=sorted_tokens)
-                else:
-                    nc.vector.tensor_copy(out=place, in_=sorted_tokens)
+        def flip(quarter, pair):
+            first = 2 * pair
+            count = min(2, TILES - first)
+            flipped = psum.tile([P, 2, count * P], F32, tag="bank")
+            by_tile = flipped[:].rearrange("q u (g k t) -> q k u g t", k=count, t=FRAMES)
+            for k in range(count):
+                transpose_words(nc, by_tile[:, k], ctx_tiles[quarter, first + k], token_order[:])
+            base = quarter * QUARTER_SAMPLES * SAMPLE_ROWS + 1 + FRAMES * first
+            samples = token_words[:, base : base + QUARTER_SAMPLES * SAMPLE_ROWS, :].rearrange(
+                "q (b r) u -> q b r u", r=SAMPLE_ROWS
+            )
+            parts = samples[:, :, 0 : SAMPLE_ROWS - 1, :].rearrange(
+                "q b (i r) u -> q b i r u", i=PARTS
+            )
+            place = parts[:, :, :, 0 : count * FRAMES, :]
+            sorted_tokens = flipped[:].rearrange(
+                "q u (b i w) -> q b i w u", b=QUARTER_SAMPLES, w=count * FRAMES
+            )
+            if quarter == 1 or quarter > 1 and pair % 2 == 1:
+                nc.vector.tensor_copy(out=place, in_=sorted_tokens)
+            else:
+                nc.scalar.copy(out=place, in_=sorted_tokens)
 
         quantised = {}
         biased = {}
@@ -251,21 +249,24 @@ def tile_timesformerlayer_pc_t_kernel(tc, ctx_s, x_res, s_out_w, s_out_b, out):
                 row = b * SAMPLE_ROWS - c * CHUNK
                 if 0 <= row < CHUNK:
                     p, j = divmod(row, RUN)
-                    nc.scalar.copy(out=biased[c][:, :, j, p : p + 1], in_=cls_mean[:, :, b : b + 1])
+                    nc.gpsimd.tensor_copy(
+                        out=biased[c][:, :, j, p : p + 1], in_=cls_mean[:, :, b : b + 1]
+                    )
 
-        def finish(c, j):
-            back = psum.tile([P, D], F32, tag="bank")
-            for m in range(D_TILES):
-                nc.tensor.transpose(
-                    back[:, m * P : (m + 1) * P], biased[c][:, m, j, :], ident[:]
+        def finish(c, half):
+            tiles = slice(2 * half, 2 * half + 2)
+            for j in range(2 * half, 2 * half + 2):
+                back = psum.tile([P, D], F32, tag="bank")
+                for m in range(D_TILES):
+                    nc.tensor.transpose(
+                        back[:, m * P : (m + 1) * P], biased[c][:, m, j, :], ident[:]
+                    )
+                nc.vector.tensor_tensor(
+                    out=finished[c][:, j, :], in0=back[:], in1=x_chunks[c][:, j, :], op=ADD
                 )
-            nc.vector.tensor_tensor(
-                out=finished[c][:, j, :], in0=back[:], in1=x_chunks[c][:, j, :], op=ADD
-            )
-
-        def store(c):
             nc.sync.dma_start(
-                out=chunk_rows(out, c), in_=finished[c][:].rearrange("p j d -> p (j d)")
+                out=chunk_rows(out, c)[:, 2 * half * D : (2 * half + 2) * D],
+                in_=finished[c][:, tiles, :].rearrange("p j d -> p (j d)"),
             )
 
         rest_codes = const.tile([P, P], U32, align_bytes=64)
@@ -302,40 +303,49 @@ def tile_timesformerlayer_pc_t_kernel(tc, ctx_s, x_res, s_out_w, s_out_b, out):
             )
             nc.sync.dma_start(out=rest_rows(out), in_=rest_out[:])
 
-        for pair in range(3):
+        for pair in range(FIRST_TILES // 2):
             flip(0, pair)
         prepare_bias()
+        for pair in range(FIRST_TILES // 2, PAIRS):
+            flip(0, pair)
         group_w()
-        for pair in range(3, 6):
-            flip(0, pair)
         quantise_w()
-        flip_class()
-        for pair in range(6, PAIRS):
-            flip(0, pair)
-        quantise_class()
         quantise(0)
-        multiply_class()
-        pairs = list(range(PAIRS))
+        flip_class()
+        quantise_class()
+        flips = {0: (1, 0, 5), 1: (2, 0, 3), 2: (2, 3, 5), 3: (3, 0, 3), 4: (3, 3, 5)}
         for c in range(CHUNKS):
             if c + 1 < CHUNKS:
                 quantise(c + 1)
-            else:
-                quantise_rest()
-            for half in range(2):
-                for m in range(2 * half, 2 * half + 2):
+            quarter, first, last = flips.get(c, (0, 0, 0))
+            middle = (first + last + 1) // 2
+            if c == 0:
+                for m in range(D_TILES):
                     multiply(c, m)
-                if half == 1:
-                    place_class(c)
-                if c > 0:
-                    for j in range(2 * half, 2 * half + 2):
-                        finish(c - 1, j)
-                if c < FLIP_CHUNKS:
-                    for pair in pairs[FLIP_PAIRS * c + 2 * half : FLIP_PAIRS * c + 2 + half]:
-                        flip(1, pair)
-            if c > 0:
-                store(c - 1)
-        multiply_rest()
-        for j in range(RUN):
-            finish(CHUNKS - 1, j)
-        store(CHUNKS - 1)
-        finish_rest()
+                multiply_class()
+                place_class(c)
+                for pair in range(first, last):
+                    flip(quarter, pair)
+            elif c in flips:
+                for half in range(2):
+                    for m in range(2 * half, 2 * half + 2):
+                        multiply(c, m)
+                    if half == 1:
+                        place_class(c)
+                    finish(c - 1, half)
+                    for pair in range(middle, last) if half else range(first, middle):
+                        flip(quarter, pair)
+            else:
+                for m in range(D_TILES):
+                    multiply(c, m)
+                place_class(c)
+                for half in range(2):
+                    finish(c - 1, half)
+            if c == CHUNKS - 3:
+                quantise_rest()
+            if c == CHUNKS - 2:
+                multiply_rest()
+            if c == CHUNKS - 1:
+                finish_rest()
+        for half in range(2):
+            finish(CHUNKS - 1, half)

@@ -249,7 +249,7 @@ def tile_timesformerlayer_pc_t_kernel(tc, ctx_s, x_res, s_out_w, s_out_b, out):
                 row = b * SAMPLE_ROWS - c * CHUNK
                 if 0 <= row < CHUNK:
                     p, j = divmod(row, RUN)
-                    nc.gpsimd.tensor_copy(
+                    nc.scalar.copy(
                         out=biased[c][:, :, j, p : p + 1], in_=cls_mean[:, :, b : b + 1]
                     )
 
@@ -257,6 +257,21 @@ def tile_timesformerlayer_pc_t_kernel(tc, ctx_s, x_res, s_out_w, s_out_b, out):
             tiles = slice(2 * half, 2 * half + 2)
             for j in range(2 * half, 2 * half + 2):
                 back = psum.tile([P, D], F32, tag="bank")
+                if c == CHUNKS - 1 and j % 2 == 0:
+                    nc.tensor.matmul(
+                        back[:], lhsT=ident_bf16[:], rhs=x_chunks[c][:, j, :], start=True, stop=False
+                    )
+                    for m in range(D_TILES):
+                        nc.tensor.matmul(
+                            back[:, m * P : (m + 1) * P],
+                            lhsT=biased[c][:, m, j, :],
+                            rhs=ident[:],
+                            is_transpose=True,
+                            start=False,
+                            stop=m == D_TILES - 1,
+                        )
+                    nc.scalar.copy(out=finished[c][:, j, :], in_=back[:])
+                    continue
                 for m in range(D_TILES):
                     nc.tensor.transpose(
                         back[:, m * P : (m + 1) * P], biased[c][:, m, j, :], ident[:]
@@ -264,10 +279,15 @@ def tile_timesformerlayer_pc_t_kernel(tc, ctx_s, x_res, s_out_w, s_out_b, out):
                 nc.vector.tensor_tensor(
                     out=finished[c][:, j, :], in0=back[:], in1=x_chunks[c][:, j, :], op=ADD
                 )
-            nc.sync.dma_start(
-                out=chunk_rows(out, c)[:, 2 * half * D : (2 * half + 2) * D],
-                in_=finished[c][:, tiles, :].rearrange("p j d -> p (j d)"),
-            )
+            if c >= 5:
+                nc.sync.dma_start(
+                    out=chunk_rows(out, c)[:, 2 * half * D : (2 * half + 2) * D],
+                    in_=finished[c][:, tiles, :].rearrange("p j d -> p (j d)"),
+                )
+            elif half == 1:
+                nc.sync.dma_start(
+                    out=chunk_rows(out, c), in_=finished[c][:].rearrange("p j d -> p (j d)")
+                )
 
         rest_codes = const.tile([P, P], U32, align_bytes=64)
         rest_scales = const.tile([P, P], U8, align_bytes=64)

@@ -77,12 +77,15 @@ def tile_timesformerlayer_pc_t_kernel(tc, ctx_s, x_res, s_out_w, s_out_b, out):
             for a in range(count):
                 ctx_tiles[quarter, first + a] = ctx_load[:, a, :]
 
-        def load_x(c):
-            x_chunk = resident.tile([P, RUN, D], BF16, name="x%d" % c)
+        def load_x(c, count):
+            x_load = resident.tile([P, count, RUN, D], BF16, name="x%d" % c)
+            rows = x_res.rearrange("b r d -> (b r) d")[c * CHUNK : (c + count) * CHUNK, :]
             nc.sync.dma_start(
-                out=x_chunk[:].rearrange("p j d -> p (j d)"), in_=chunk_rows(x_res, c)
+                out=x_load[:].rearrange("p c j d -> p c (j d)"),
+                in_=rows.rearrange("(c p j) d -> p c (j d)", p=P, j=RUN),
             )
-            x_chunks.append(x_chunk)
+            for i in range(count):
+                x_chunks.append(x_load[:, i])
 
         load_ctx(0, 0, FIRST_TILES)
         nc.sync.dma_start(
@@ -93,11 +96,13 @@ def tile_timesformerlayer_pc_t_kernel(tc, ctx_s, x_res, s_out_w, s_out_b, out):
         nc.sync.dma_start(out=w_rows[:], in_=s_out_w.rearrange("(q v) c -> q v c", v=PACK))
         cls_ctx = resident.tile([P, D], BF16)
         nc.sync.dma_start(out=cls_ctx[:], in_=ctx_s[:, 0, :])
-        for quarter in range(1, QUARTERS):
-            load_ctx(quarter, 0, TILES)
-            load_x(quarter - 1)
-        for c in range(QUARTERS - 1, CHUNKS):
-            load_x(c)
+        load_ctx(1, 0, TILES)
+        load_x(0, 1)
+        load_ctx(2, 0, TILES)
+        load_x(1, 2)
+        load_ctx(3, 0, TILES)
+        for c in range(3, CHUNKS, 2):
+            load_x(c, 2)
         rest_x = resident.tile([REST, D], BF16)
         nc.sync.dma_start(out=rest_x[:], in_=rest_rows(x_res))
 
@@ -174,6 +179,11 @@ def tile_timesformerlayer_pc_t_kernel(tc, ctx_s, x_res, s_out_w, s_out_b, out):
             for m in range(D_TILES):
                 multiply_by_w(prod[:, m, :], m, codes, scales)
             return prod
+
+        def warm_up():
+            unread = psum.tile([P, D], F32, tag="bank")
+            for i in range(3):
+                nc.tensor.matmul(unread[:], lhsT=ident_bf16[:], rhs=cls_ctx[:], start=True, stop=True)
 
         def multiply_class():
             cls_prod = multiply_128(cls_codes[:], cls_scales[:])
@@ -330,8 +340,9 @@ def tile_timesformerlayer_pc_t_kernel(tc, ctx_s, x_res, s_out_w, s_out_b, out):
             flip(0, pair)
         group_w()
         quantise_w()
-        quantise(0)
         flip_class()
+        warm_up()
+        quantise(0)
         quantise_class()
         flips = {0: (1, 0, 5), 1: (2, 0, 3), 2: (2, 3, 5), 3: (3, 0, 3), 4: (3, 3, 5)}
         for c in range(CHUNKS):

@@ -24,7 +24,7 @@ QUARTER_SAMPLES = SAMPLES // QUARTERS
 PARTS = 4
 TILES = PATCHES // PARTS
 PAIRS = (TILES + 1) // 2
-FIRST_TILES = 4
+HEAD_LOADS = (4, 4, 1)
 SAMPLE_ROWS = 1 + FRAMES * PATCHES
 ROWS = SAMPLES * SAMPLE_ROWS
 RUN = 4
@@ -87,11 +87,12 @@ def tile_timesformerlayer_pc_t_kernel(tc, ctx_s, x_res, s_out_w, s_out_b, out):
             for i in range(count):
                 x_chunks.append(x_load[:, i])
 
-        load_ctx(0, 0, FIRST_TILES)
-        nc.sync.dma_start(
-            out=bias_rows[0:D_TILES, :], in_=s_out_b.rearrange("(m d) -> m d", m=D_TILES)
-        )
-        load_ctx(0, FIRST_TILES, TILES - FIRST_TILES)
+        for i, count in enumerate(HEAD_LOADS):
+            load_ctx(0, sum(HEAD_LOADS[:i]), count)
+            if i == 0:
+                nc.sync.dma_start(
+                    out=bias_rows[0:D_TILES, :], in_=s_out_b.rearrange("(m d) -> m d", m=D_TILES)
+                )
         w_rows = const.tile([P, PACK, D], BF16)
         nc.sync.dma_start(out=w_rows[:], in_=s_out_w.rearrange("(q v) c -> q v c", v=PACK))
         cls_ctx = resident.tile([P, D], BF16)
@@ -123,6 +124,9 @@ def tile_timesformerlayer_pc_t_kernel(tc, ctx_s, x_res, s_out_w, s_out_b, out):
         rest_biased = const.tile([P, D_TILES, P], F32)
         nc.vector.memset(rest_biased[:], 0.0)
 
+        zeros = const.tile([P, D], BF16)
+        nc.gpsimd.memset(zeros[:], 0.0)
+
         bias_col = const.tile([P, D_TILES], F32)
         w_grouped = const.tile([P, D, PACK], BF16, align_bytes=64)
         w_codes = const.tile([P, D], U32, align_bytes=64)
@@ -133,14 +137,18 @@ def tile_timesformerlayer_pc_t_kernel(tc, ctx_s, x_res, s_out_w, s_out_b, out):
             nc.tensor.transpose(bias_flipped[:], bias_rows[:], ident_bf16[:])
             nc.scalar.copy(out=bias_col[:], in_=bias_flipped[:, 0:D_TILES])
 
-        def group_w():
-            nc.vector.tensor_copy(out=w_grouped[:], in_=w_rows[:].rearrange("q v c -> q c v"))
+        def group_w(m):
+            columns = slice(m * P, (m + 1) * P)
+            nc.vector.tensor_copy(
+                out=w_grouped[:, columns, :], in_=w_rows[:, :, columns].rearrange("q v c -> q c v")
+            )
 
-        def quantise_w():
+        def quantise_w(m):
+            columns = slice(m * P, (m + 1) * P)
             nc.vector.quantize_mx(
-                out=w_codes[:].bitcast(FP8X4),
-                scales=w_scales[:],
-                in_=w_grouped[:].rearrange("q c v -> q (c v)"),
+                out=w_codes[:, columns].bitcast(FP8X4),
+                scales=w_scales[:, columns],
+                in_=w_grouped[:, columns, :].rearrange("q c v -> q (c v)"),
             )
 
         def multiply_by_w(prod, m, codes, scales):
@@ -183,7 +191,7 @@ def tile_timesformerlayer_pc_t_kernel(tc, ctx_s, x_res, s_out_w, s_out_b, out):
         def warm_up():
             unread = psum.tile([P, D], F32, tag="bank")
             for i in range(3):
-                nc.tensor.matmul(unread[:], lhsT=ident_bf16[:], rhs=cls_ctx[:], start=True, stop=True)
+                nc.tensor.matmul(unread[:], lhsT=ident_bf16[:], rhs=zeros[:], start=True, stop=True)
 
         def multiply_class():
             cls_prod = multiply_128(cls_codes[:], cls_scales[:])
@@ -333,16 +341,21 @@ def tile_timesformerlayer_pc_t_kernel(tc, ctx_s, x_res, s_out_w, s_out_b, out):
             )
             nc.sync.dma_start(out=rest_rows(out), in_=rest_out[:])
 
-        for pair in range(FIRST_TILES // 2):
+        for pair in range(PAIRS):
             flip(0, pair)
-        prepare_bias()
-        for pair in range(FIRST_TILES // 2, PAIRS):
-            flip(0, pair)
-        group_w()
-        quantise_w()
-        flip_class()
+            if pair == 1:
+                prepare_bias()
         warm_up()
+        flip_class()
+        group_w(0)
+        group_w(1)
+        quantise_w(0)
         quantise(0)
+        quantise_w(1)
+        group_w(2)
+        group_w(3)
+        quantise_w(2)
+        quantise_w(3)
         quantise_class()
         flips = {0: (1, 0, 5), 1: (2, 0, 3), 2: (2, 3, 5), 3: (3, 0, 3), 4: (3, 3, 5)}
         for c in range(CHUNKS):

@@ -362,7 +362,6 @@ def tile_timesformerlayer_pc_t_kernel(tc, ctx_s, x_res, s_out_w, s_out_b, out):
             if c + 1 < CHUNKS:
                 quantise(c + 1)
             quarter, first, last = flips.get(c, (0, 0, 0))
-            middle = (first + last + 1) // 2
             if c == 0:
                 for m in range(D_TILES):
                     multiply(c, m)
@@ -371,14 +370,13 @@ def tile_timesformerlayer_pc_t_kernel(tc, ctx_s, x_res, s_out_w, s_out_b, out):
                 for pair in range(first, last):
                     flip(quarter, pair)
             elif c in flips:
+                for m in range(D_TILES):
+                    multiply(c, m)
+                place_class(c)
                 for half in range(2):
-                    for m in range(2 * half, 2 * half + 2):
-                        multiply(c, m)
-                    if half == 1:
-                        place_class(c)
                     finish(c - 1, half)
-                    for pair in range(middle, last) if half else range(first, middle):
-                        flip(quarter, pair)
+                for pair in range(first, last):
+                    flip(quarter, pair)
             else:
                 for m in range(D_TILES):
                     multiply(c, m)

@@ -24,7 +24,8 @@ QUARTER_SAMPLES = SAMPLES // QUARTERS
 PARTS = 4
 TILES = PATCHES // PARTS
 PAIRS = (TILES + 1) // 2
-HEAD_LOADS = (4, 4, 1)
+VECTOR_FLIPS = ((0, 3), (1, 2), (1, 3), (1, 4), (2, 1), (3, 1))
+HEAD_LOADS = (4, 5)
 SAMPLE_ROWS = 1 + FRAMES * PATCHES
 ROWS = SAMPLES * SAMPLE_ROWS
 RUN = 4
@@ -93,11 +94,12 @@ def tile_timesformerlayer_pc_t_kernel(tc, ctx_s, x_res, s_out_w, s_out_b, out):
                 nc.sync.dma_start(
                     out=bias_rows[0:D_TILES, :], in_=s_out_b.rearrange("(m d) -> m d", m=D_TILES)
                 )
+        load_ctx(1, 0, HEAD_LOADS[0])
         w_rows = const.tile([P, PACK, D], BF16)
         nc.sync.dma_start(out=w_rows[:], in_=s_out_w.rearrange("(q v) c -> q v c", v=PACK))
         cls_ctx = resident.tile([P, D], BF16)
         nc.sync.dma_start(out=cls_ctx[:], in_=ctx_s[:, 0, :])
-        load_ctx(1, 0, TILES)
+        load_ctx(1, HEAD_LOADS[0], HEAD_LOADS[1])
         load_x(0, 1)
         load_ctx(2, 0, TILES)
         load_x(1, 2)
@@ -139,9 +141,12 @@ def tile_timesformerlayer_pc_t_kernel(tc, ctx_s, x_res, s_out_w, s_out_b, out):
 
         def group_w(m):
             columns = slice(m * P, (m + 1) * P)
-            nc.vector.tensor_copy(
-                out=w_grouped[:, columns, :], in_=w_rows[:, :, columns].rearrange("q v c -> q c v")
-            )
+            place = w_grouped[:, columns, :]
+            rows = w_rows[:, :, columns].rearrange("q v c -> q c v")
+            if m == D_TILES - 1:
+                nc.scalar.copy(out=place, in_=rows)
+            else:
+                nc.vector.tensor_copy(out=place, in_=rows)
 
         def quantise_w(m):
             columns = slice(m * P, (m + 1) * P)
@@ -190,7 +195,7 @@ def tile_timesformerlayer_pc_t_kernel(tc, ctx_s, x_res, s_out_w, s_out_b, out):
 
         def warm_up():
             unread = psum.tile([P, D], F32, tag="bank")
-            for i in range(3):
+            for i in range(2):
                 nc.tensor.matmul(unread[:], lhsT=ident_bf16[:], rhs=zeros[:], start=True, stop=True)
 
         def multiply_class():
@@ -229,7 +234,7 @@ def tile_timesformerlayer_pc_t_kernel(tc, ctx_s, x_res, s_out_w, s_out_b, out):
             sorted_tokens = flipped[:].rearrange(
                 "q u (b i w) -> q b i w u", b=QUARTER_SAMPLES, w=count * FRAMES
             )
-            if quarter == 1 or quarter > 1 and pair % 2 == 1:
+            if (quarter, pair) in VECTOR_FLIPS:
                 nc.vector.tensor_copy(out=place, in_=sorted_tokens)
             else:
                 nc.scalar.copy(out=place, in_=sorted_tokens)
@@ -345,25 +350,27 @@ def tile_timesformerlayer_pc_t_kernel(tc, ctx_s, x_res, s_out_w, s_out_b, out):
             flip(0, pair)
             if pair == 1:
                 prepare_bias()
-        warm_up()
+        group_w(3)
+        for pair in range(2):
+            flip(1, pair)
         flip_class()
+        warm_up()
+        quantise(0)
         group_w(0)
         group_w(1)
         quantise_w(0)
-        quantise(0)
         quantise_w(1)
-        group_w(2)
-        group_w(3)
-        quantise_w(2)
         quantise_w(3)
+        group_w(2)
         quantise_class()
-        flips = {0: (1, 0, 5), 1: (2, 0, 3), 2: (2, 3, 5), 3: (3, 0, 3), 4: (3, 3, 5)}
+        quantise_w(2)
+        flips = {0: (1, 2, 5), 1: (2, 0, 3), 2: (2, 3, 5), 3: (3, 0, 3), 4: (3, 3, 5)}
         for c in range(CHUNKS):
             if c + 1 < CHUNKS:
                 quantise(c + 1)
             quarter, first, last = flips.get(c, (0, 0, 0))
             if c == 0:
-                for m in range(D_TILES):
+                for m in (0, 1, 3, 2):
                     multiply(c, m)
                 multiply_class()
                 place_class(c)

@@ -68,7 +68,9 @@ def tile_timesformerlayer_pc_t_kernel(tc, ctx_s, x_res, s_out_w, s_out_b, out):
         x_chunks = []
 
         def load_ctx(quarter, first, count):
-            ctx_load = resident.tile([P, count, D], BF16, name="ctx%d%d" % (quarter, first))
+            ctx_load = resident.tile(
+                [P, count, D], BF16, name="ctx%d%d" % (quarter, first), align_bytes=256
+            )
             sequences = ctx_s[quarter * P // PARTS : (quarter + 1) * P // PARTS, 1:, :]
             patches = sequences.rearrange("s (i a) d -> s i a d", i=PARTS)
             nc.sync.dma_start(
@@ -79,7 +81,7 @@ def tile_timesformerlayer_pc_t_kernel(tc, ctx_s, x_res, s_out_w, s_out_b, out):
                 ctx_tiles[quarter, first + a] = ctx_load[:, a, :]
 
         def load_x(c, count):
-            x_load = resident.tile([P, count, RUN, D], BF16, name="x%d" % c)
+            x_load = resident.tile([P, count, RUN, D], BF16, name="x%d" % c, align_bytes=256)
             rows = x_res.rearrange("b r d -> (b r) d")[c * CHUNK : (c + count) * CHUNK, :]
             nc.sync.dma_start(
                 out=x_load[:].rearrange("p c j d -> p c (j d)"),
@@ -95,9 +97,9 @@ def tile_timesformerlayer_pc_t_kernel(tc, ctx_s, x_res, s_out_w, s_out_b, out):
                     out=bias_rows[0:D_TILES, :], in_=s_out_b.rearrange("(m d) -> m d", m=D_TILES)
                 )
         load_ctx(1, 0, HEAD_LOADS[0])
-        w_rows = const.tile([P, PACK, D], BF16)
+        w_rows = const.tile([P, PACK, D], BF16, align_bytes=256)
         nc.sync.dma_start(out=w_rows[:], in_=s_out_w.rearrange("(q v) c -> q v c", v=PACK))
-        cls_ctx = resident.tile([P, D], BF16)
+        cls_ctx = resident.tile([P, D], BF16, align_bytes=256)
         nc.sync.dma_start(out=cls_ctx[:], in_=ctx_s[:, 0, :])
         load_ctx(1, HEAD_LOADS[0], HEAD_LOADS[1])
         load_x(0, 1)
@@ -253,7 +255,7 @@ def tile_timesformerlayer_pc_t_kernel(tc, ctx_s, x_res, s_out_w, s_out_b, out):
             )
             quantised[c] = (codes, scales)
             biased[c] = work.tile([P, D_TILES, RUN, P], F32, name="with_bias")
-            finished[c] = stores.tile([P, RUN, D], F32, name="out_chunk")
+            finished[c] = stores.tile([P, RUN, D], F32, name="out_chunk", align_bytes=256)
 
         def multiply(c, m):
             codes, scales = quantised[c]

@@ -62,7 +62,7 @@ def tile_timesformerlayer_pc_t_kernel(tc, ctx_s, x_res, s_out_w, s_out_b, out):
         psum = scope.enter_context(tc.psum_pool(name="psum", bufs=8))
         scope.enter_context(tc.manual_schedule())
 
-        bias_rows = const.tile([P, P], BF16)
+        bias_rows = const.tile([P, P], BF16, align_bytes=256)
         nc.vector.memset(bias_rows[:], 0.0)
         ctx_tiles = {}
         x_chunks = []
@@ -108,33 +108,33 @@ def tile_timesformerlayer_pc_t_kernel(tc, ctx_s, x_res, s_out_w, s_out_b, out):
         load_ctx(3, 0, TILES)
         for c in range(3, CHUNKS, 2):
             load_x(c, 2)
-        rest_x = resident.tile([REST, D], BF16)
+        rest_x = resident.tile([REST, D], BF16, align_bytes=256)
         nc.sync.dma_start(out=rest_x[:], in_=rest_rows(x_res))
 
-        tokens = resident.tile([P, TOKENS, PACK], BF16, align_bytes=64)
+        tokens = resident.tile([P, TOKENS, PACK], BF16, align_bytes=256)
         token_words = tokens[:].bitcast(F32)
         samples = tokens[:, 0:ROWS, :].rearrange("q (b r) v -> q b r v", r=SAMPLE_ROWS)
         nc.vector.memset(samples[:, :, 0, :], 0.0)
         nc.vector.memset(tokens[:, ROWS : CHUNKS * CHUNK + P, :], 0.0)
-        ident = const.tile([P, P], F32)
+        ident = const.tile([P, P], F32, align_bytes=256)
         make_identity(nc, ident[:])
-        token_order = const.tile([P, P], F32)
+        token_order = const.tile([P, P], F32, align_bytes=256)
         nc.vector.tensor_copy(
             out=token_order[:].rearrange("n (b i t) -> n b i t", i=PARTS, t=FRAMES),
             in_=ident[:].rearrange("n (b t i) -> n b i t", i=PARTS, t=FRAMES),
         )
-        ident_bf16 = const.tile([P, P], BF16)
+        ident_bf16 = const.tile([P, P], BF16, align_bytes=256)
         nc.vector.tensor_copy(out=ident_bf16[:], in_=ident[:])
-        rest_biased = const.tile([P, D_TILES, P], F32)
+        rest_biased = const.tile([P, D_TILES, P], F32, align_bytes=256)
         nc.vector.memset(rest_biased[:], 0.0)
 
-        zeros = const.tile([P, D], BF16)
+        zeros = const.tile([P, D], BF16, align_bytes=256)
         nc.gpsimd.memset(zeros[:], 0.0)
 
-        bias_col = const.tile([P, D_TILES], F32)
-        w_grouped = const.tile([P, D, PACK], BF16, align_bytes=64)
-        w_codes = const.tile([P, D], U32, align_bytes=64)
-        w_scales = const.tile([P, D], U8, align_bytes=64)
+        bias_col = const.tile([P, D_TILES], F32, align_bytes=256)
+        w_grouped = const.tile([P, D, PACK], BF16, align_bytes=256)
+        w_codes = const.tile([P, D], U32, align_bytes=256)
+        w_scales = const.tile([P, D], U8, align_bytes=256)
 
         def prepare_bias():
             bias_flipped = psum.tile([P, P], BF16, tag="bank")
@@ -170,10 +170,10 @@ def tile_timesformerlayer_pc_t_kernel(tc, ctx_s, x_res, s_out_w, s_out_b, out):
                 stop=True,
             )
 
-        cls_grouped = const.tile([P, P, PACK], BF16, align_bytes=64)
-        cls_codes = const.tile([P, P], U32, align_bytes=64)
-        cls_scales = const.tile([P, P], U8, align_bytes=64)
-        cls_mean = const.tile([P, D_TILES, SAMPLES], F32)
+        cls_grouped = const.tile([P, P, PACK], BF16, align_bytes=256)
+        cls_codes = const.tile([P, P], U32, align_bytes=256)
+        cls_scales = const.tile([P, P], U8, align_bytes=256)
+        cls_mean = const.tile([P, D_TILES, SAMPLES], F32, align_bytes=256)
 
         def flip_class():
             cls_flipped = psum.tile([P, 2, P], F32, tag="bank")
@@ -202,7 +202,7 @@ def tile_timesformerlayer_pc_t_kernel(tc, ctx_s, x_res, s_out_w, s_out_b, out):
 
         def multiply_class():
             cls_prod = multiply_128(cls_codes[:], cls_scales[:])
-            cls_sum = const.tile([P, D_TILES, SAMPLES], F32)
+            cls_sum = const.tile([P, D_TILES, SAMPLES], F32, align_bytes=256)
             nc.vector.tensor_reduce(
                 out=cls_sum[:],
                 in_=cls_prod[:].rearrange("i m (b t) -> i m b t", t=FRAMES),
@@ -246,15 +246,15 @@ def tile_timesformerlayer_pc_t_kernel(tc, ctx_s, x_res, s_out_w, s_out_b, out):
         finished = {}
 
         def quantise(c):
-            codes = work.tile([P, CHUNK], U32, align_bytes=64)
-            scales = work.tile([P, CHUNK], U8, align_bytes=64)
+            codes = work.tile([P, CHUNK], U32, align_bytes=256)
+            scales = work.tile([P, CHUNK], U8, align_bytes=256)
             nc.vector.quantize_mx(
                 out=codes[:].bitcast(FP8X4),
                 scales=scales[:],
                 in_=tokens[:, c * CHUNK : (c + 1) * CHUNK, :].rearrange("q r v -> q (r v)"),
             )
             quantised[c] = (codes, scales)
-            biased[c] = work.tile([P, D_TILES, RUN, P], F32, name="with_bias")
+            biased[c] = work.tile([P, D_TILES, RUN, P], F32, name="with_bias", align_bytes=256)
             finished[c] = stores.tile([P, RUN, D], F32, name="out_chunk", align_bytes=256)
 
         def multiply(c, m):
@@ -314,8 +314,8 @@ def tile_timesformerlayer_pc_t_kernel(tc, ctx_s, x_res, s_out_w, s_out_b, out):
                     out=chunk_rows(out, c), in_=finished[c][:].rearrange("p j d -> p (j d)")
                 )
 
-        rest_codes = const.tile([P, P], U32, align_bytes=64)
-        rest_scales = const.tile([P, P], U8, align_bytes=64)
+        rest_codes = const.tile([P, P], U32, align_bytes=256)
+        rest_scales = const.tile([P, P], U8, align_bytes=256)
 
         def quantise_rest():
             first = CHUNKS * CHUNK
@@ -342,7 +342,7 @@ def tile_timesformerlayer_pc_t_kernel(tc, ctx_s, x_res, s_out_w, s_out_b, out):
                 nc.tensor.transpose(
                     rest_back[:, m * P : (m + 1) * P], rest_biased[:, m, :], ident[:]
                 )
-            rest_out = const.tile([REST, D], F32)
+            rest_out = const.tile([REST, D], F32, align_bytes=256)
             nc.vector.tensor_tensor(
                 out=rest_out[:], in0=rest_back[0:REST, :], in1=rest_x[:], op=ADD
             )

@@ -57,8 +57,8 @@ def tile_timesformerlayer_pc_t_kernel(tc, ctx_s, x_res, s_out_w, s_out_b, out):
     with ExitStack() as scope:
         const = scope.enter_context(tc.tile_pool(name="const", bufs=1))
         resident = scope.enter_context(tc.tile_pool(name="resident", bufs=1))
-        work = scope.enter_context(tc.tile_pool(name="work", bufs=3))
-        stores = scope.enter_context(tc.tile_pool(name="stores", bufs=6))
+        work = scope.enter_context(tc.tile_pool(name="work", bufs=2))
+        stores = scope.enter_context(tc.tile_pool(name="stores", bufs=5))
         psum = scope.enter_context(tc.psum_pool(name="psum", bufs=8))
         scope.enter_context(tc.manual_schedule())
 
@@ -69,7 +69,7 @@ def tile_timesformerlayer_pc_t_kernel(tc, ctx_s, x_res, s_out_w, s_out_b, out):
 
         def load_ctx(quarter, first, count):
             ctx_load = resident.tile(
-                [P, count, D], BF16, name="ctx%d%d" % (quarter, first), align_bytes=256
+                [P, count, D], BF16, name="ctx%d%d" % (quarter, first), align_bytes=1024
             )
             sequences = ctx_s[quarter * P // PARTS : (quarter + 1) * P // PARTS, 1:, :]
             patches = sequences.rearrange("s (i a) d -> s i a d", i=PARTS)
@@ -81,7 +81,7 @@ def tile_timesformerlayer_pc_t_kernel(tc, ctx_s, x_res, s_out_w, s_out_b, out):
                 ctx_tiles[quarter, first + a] = ctx_load[:, a, :]
 
         def load_x(c, count):
-            x_load = resident.tile([P, count, RUN, D], BF16, name="x%d" % c, align_bytes=256)
+            x_load = resident.tile([P, count, RUN, D], BF16, name="x%d" % c, align_bytes=4096)
             rows = x_res.rearrange("b r d -> (b r) d")[c * CHUNK : (c + count) * CHUNK, :]
             nc.sync.dma_start(
                 out=x_load[:].rearrange("p c j d -> p c (j d)"),
@@ -255,7 +255,7 @@ def tile_timesformerlayer_pc_t_kernel(tc, ctx_s, x_res, s_out_w, s_out_b, out):
             )
             quantised[c] = (codes, scales)
             biased[c] = work.tile([P, D_TILES, RUN, P], F32, name="with_bias", align_bytes=256)
-            finished[c] = stores.tile([P, RUN, D], F32, name="out_chunk", align_bytes=256)
+            finished[c] = stores.tile([P, RUN, D], F32, name="out_chunk", align_bytes=4096)
 
         def multiply(c, m):
             codes, scales = quantised[c]

from contextlib import ExitStack

import concourse.mybir as mybir
from concourse.masks import make_identity

F32 = mybir.dt.float32
BF16 = mybir.dt.bfloat16
U32 = mybir.dt.uint32
U8 = mybir.dt.uint8
FP8X4 = mybir.dt.float8_e4m3fn_x4
ADD = mybir.AluOpType.add
IDENTITY = mybir.ActivationFunctionType.Identity

P = 128
PACK = 4
SAMPLES = 16
FRAMES = 8
PATCHES = 36
D = 512
D_TILES = D // P

QUARTERS = 4
QUARTER_SAMPLES = SAMPLES // QUARTERS
PARTS = 4
TILES = PATCHES // PARTS
PAIRS = (TILES + 1) // 2
VECTOR_FLIPS = ((0, 3), (1, 2), (1, 3), (1, 4), (2, 1), (3, 1))
HEAD_LOADS = (4, 5)
SAMPLE_ROWS = 1 + FRAMES * PATCHES
ROWS = SAMPLES * SAMPLE_ROWS
RUN = 4
CHUNK = RUN * P
CHUNKS = ROWS // CHUNK
REST = ROWS - CHUNKS * CHUNK
TOKENS = ROWS + SAMPLE_ROWS

FLOPS = 2 * SAMPLES * FRAMES * (1 + PATCHES) * D * D


def transpose_words(nc, flipped, rows, permutation):
    words = rows.bitcast(F32)
    for u in range(2):
        nc.tensor.transpose(flipped[:, u, :], words[:, u::2], permutation)


def chunk_rows(tensor, c):
    rows = tensor.rearrange("b r d -> (b r) d")[c * CHUNK : (c + 1) * CHUNK, :]
    return rows.rearrange("(p j) d -> p (j d)", j=RUN)


def rest_rows(tensor):
    return tensor[SAMPLES - 1, SAMPLE_ROWS - REST :, :]


def tile_timesformerlayer_pc_t_kernel(tc, ctx_s, x_res, s_out_w, s_out_b, out):
    nc = tc.nc
    with ExitStack() as scope:
        const = scope.enter_context(tc.tile_pool(name="const", bufs=1))
        resident = scope.enter_context(tc.tile_pool(name="resident", bufs=1))
        work = scope.enter_context(tc.tile_pool(name="work", bufs=2))
        stores = scope.enter_context(tc.tile_pool(name="stores", bufs=5))
        psum = scope.enter_context(tc.psum_pool(name="psum", bufs=8))
        scope.enter_context(tc.manual_schedule())

        bias_rows = const.tile([P, P], BF16, align_bytes=256)
        nc.vector.memset(bias_rows[:], 0.0)
        ctx_tiles = {}
        x_chunks = []

        def load_ctx(quarter, first, count):
            ctx_load = resident.tile(
                [P, count, D], BF16, name="ctx%d%d" % (quarter, first), align_bytes=1024
            )
            sequences = ctx_s[quarter * P // PARTS : (quarter + 1) * P // PARTS, 1:, :]
            patches = sequences.rearrange("s (i a) d -> s i a d", i=PARTS)
            nc.sync.dma_start(
                out=ctx_load[:].rearrange("n a d -> n (a d)"),
                in_=patches[:, :, first : first + count, :].rearrange("s i a d -> s i (a d)"),
            )
            for a in range(count):
                ctx_tiles[quarter, first + a] = ctx_load[:, a, :]

        def load_x(c, count):
            x_load = resident.tile([P, count, RUN, D], BF16, name="x%d" % c, align_bytes=4096)
            rows = x_res.rearrange("b r d -> (b r) d")[c * CHUNK : (c + count) * CHUNK, :]
            nc.sync.dma_start(
                out=x_load[:].rearrange("p c j d -> p c (j d)"),
                in_=rows.rearrange("(c p j) d -> p c (j d)", p=P, j=RUN),
            )
            for i in range(count):
                x_chunks.append(x_load[:, i])

        for i, count in enumerate(HEAD_LOADS):
            load_ctx(0, sum(HEAD_LOADS[:i]), count)
            if i == 0:
                nc.sync.dma_start(
                    out=bias_rows[0:D_TILES, :], in_=s_out_b.rearrange("(m d) -> m d", m=D_TILES)
                )
        load_ctx(1, 0, HEAD_LOADS[0])
        w_rows = const.tile([P, PACK, D], BF16, align_bytes=256)
        nc.sync.dma_start(out=w_rows[:], in_=s_out_w.rearrange("(q v) c -> q v c", v=PACK))
        cls_ctx = resident.tile([P, D], BF16, align_bytes=256)
        nc.sync.dma_start(out=cls_ctx[:], in_=ctx_s[:, 0, :])
        load_ctx(1, HEAD_LOADS[0], HEAD_LOADS[1])
        load_x(0, 1)
        load_ctx(2, 0, TILES)
        load_x(1, 2)
        load_ctx(3, 0, TILES)
        for c in range(3, CHUNKS, 2):
            load_x(c, 2)
        rest_x = resident.tile([REST, D], BF16, align_bytes=256)
        nc.sync.dma_start(out=rest_x[:], in_=rest_rows(x_res))

        tokens = resident.tile([P, TOKENS, PACK], BF16, align_bytes=256)
        token_words = tokens[:].bitcast(F32)
        samples = tokens[:, 0:ROWS, :].rearrange("q (b r) v -> q b r v", r=SAMPLE_ROWS)
        nc.vector.memset(samples[:, :, 0, :], 0.0)
        nc.vector.memset(tokens[:, ROWS : CHUNKS * CHUNK + P, :], 0.0)
        ident = const.tile([P, P], F32, align_bytes=256)
        make_identity(nc, ident[:])
        token_order = const.tile([P, P], F32, align_bytes=256)
        nc.vector.tensor_copy(
            out=token_order[:].rearrange("n (b i t) -> n b i t", i=PARTS, t=FRAMES),
            in_=ident[:].rearrange("n (b t i) -> n b i t", i=PARTS, t=FRAMES),
        )
        ident_bf16 = const.tile([P, P], BF16, align_bytes=256)
        nc.vector.tensor_copy(out=ident_bf16[:], in_=ident[:])
        rest_biased = const.tile([P, D_TILES, P], F32, align_bytes=256)
        nc.vector.memset(rest_biased[:], 0.0)

        zeros = const.tile([P, D], BF16, align_bytes=256)
        nc.gpsimd.memset(zeros[:], 0.0)

        bias_col = const.tile([P, D_TILES], F32, align_bytes=256)
        w_grouped = const.tile([P, D, PACK], BF16, align_bytes=256)
        w_codes = const.tile([P, D], U32, align_bytes=256)
        w_scales = const.tile([P, D], U8, align_bytes=256)

        def prepare_bias():
            bias_flipped = psum.tile([P, P], BF16, tag="bank")
            nc.tensor.transpose(bias_flipped[:], bias_rows[:], ident_bf16[:])
            nc.scalar.copy(out=bias_col[:], in_=bias_flipped[:, 0:D_TILES])

        def group_w(m):
            columns = slice(m * P, (m + 1) * P)
            place = w_grouped[:, columns, :]
            rows = w_rows[:, :, columns].rearrange("q v c -> q c v")
            if m == D_TILES - 1:
                nc.scalar.copy(out=place, in_=rows)
            else:
                nc.vector.tensor_copy(out=place, in_=rows)

        def quantise_w(m):
            columns = slice(m * P, (m + 1) * P)
            nc.vector.quantize_mx(
                out=w_codes[:, columns].bitcast(FP8X4),
                scales=w_scales[:, columns],
                in_=w_grouped[:, columns, :].rearrange("q c v -> q (c v)"),
            )

        def multiply_by_w(prod, m, codes, scales):
            columns = slice(m * P, (m + 1) * P)
            nc.tensor.matmul_mx(
                out=prod,
                lhsT=w_codes[:, columns].bitcast(FP8X4),
                lhsT_scale=w_scales[:, columns],
                rhs=codes.bitcast(FP8X4),
                rhs_scale=scales,
                start=True,
                stop=True,
            )

        cls_grouped = const.tile([P, P, PACK], BF16, align_bytes=256)
        cls_codes = const.tile([P, P], U32, align_bytes=256)
        cls_scales = const.tile([P, P], U8, align_bytes=256)
        cls_mean = const.tile([P, D_TILES, SAMPLES], F32, align_bytes=256)

        def flip_class():
            cls_flipped = psum.tile([P, 2, P], F32, tag="bank")
            transpose_words(nc, cls_flipped, cls_ctx[:], ident[:])
            nc.scalar.copy(
                out=cls_grouped[:].bitcast(F32), in_=cls_flipped[:].rearrange("q u n -> q n u")
            )

        def quantise_class():
            nc.vector.quantize_mx(
                out=cls_codes[:].bitcast(FP8X4),
                scales=cls_scales[:],
                in_=cls_grouped[:].rearrange("q n v -> q (n v)"),
            )

        def multiply_128(codes, scales):
            prod = psum.tile([P, D_TILES, P], F32, tag="bank")
            for m in range(D_TILES):
                multiply_by_w(prod[:, m, :], m, codes, scales)
            return prod

        def warm_up():
            unread = psum.tile([P, D], F32, tag="bank")
            for i in range(2):
                nc.tensor.matmul(unread[:], lhsT=ident_bf16[:], rhs=zeros[:], start=True, stop=True)

        def multiply_class():
            cls_prod = multiply_128(cls_codes[:], cls_scales[:])
            cls_sum = const.tile([P, D_TILES, SAMPLES], F32, align_bytes=256)
            nc.vector.tensor_reduce(
                out=cls_sum[:],
                in_=cls_prod[:].rearrange("i m (b t) -> i m b t", t=FRAMES),
                axis=mybir.AxisListType.X,
                op=ADD,
            )
            for m in range(D_TILES):
                nc.scalar.activation(
                    out=cls_mean[:, m, :],
                    in_=cls_sum[:, m, :],
                    func=IDENTITY,
                    bias=bias_col[:, m : m + 1],
                    scale=1.0 / FRAMES,
                )

        def flip(quarter, pair):
            first = 2 * pair
            count = min(2, TILES - first)
            flipped = psum.tile([P, 2, count * P], F32, tag="bank")
            by_tile = flipped[:].rearrange("q u (g k t) -> q k u g t", k=count, t=FRAMES)
            for k in range(count):
                transpose_words(nc, by_tile[:, k], ctx_tiles[quarter, first + k], token_order[:])
            base = quarter * QUARTER_SAMPLES * SAMPLE_ROWS + 1 + FRAMES * first
            samples = token_words[:, base : base + QUARTER_SAMPLES * SAMPLE_ROWS, :].rearrange(
                "q (b r) u -> q b r u", r=SAMPLE_ROWS
            )
            parts = samples[:, :, 0 : SAMPLE_ROWS - 1, :].rearrange(
                "q b (i r) u -> q b i r u", i=PARTS
            )
            place = parts[:, :, :, 0 : count * FRAMES, :]
            sorted_tokens = flipped[:].rearrange(
                "q u (b i w) -> q b i w u", b=QUARTER_SAMPLES, w=count * FRAMES
            )
            if (quarter, pair) in VECTOR_FLIPS:
                nc.vector.tensor_copy(out=place, in_=sorted_tokens)
            else:
                nc.scalar.copy(out=place, in_=sorted_tokens)

        quantised = {}
        biased = {}
        finished = {}

        def quantise(c):
            codes = work.tile([P, CHUNK], U32, align_bytes=256)
            scales = work.tile([P, CHUNK], U8, align_bytes=256)
            nc.vector.quantize_mx(
                out=codes[:].bitcast(FP8X4),
                scales=scales[:],
                in_=tokens[:, c * CHUNK : (c + 1) * CHUNK, :].rearrange("q r v -> q (r v)"),
            )
            quantised[c] = (codes, scales)
            biased[c] = work.tile([P, D_TILES, RUN, P], F32, name="with_bias", align_bytes=256)
            finished[c] = stores.tile([P, RUN, D], F32, name="out_chunk", align_bytes=4096)

        def multiply(c, m):
            codes, scales = quantised[c]
            prod = psum.tile([P, CHUNK], F32, tag="bank")
            multiply_by_w(prod[:], m, codes[:], scales[:])
            nc.scalar.activation(
                out=biased[c][:, m, :, :],
                in_=prod[:].rearrange("i (p j) -> i j p", j=RUN),
                func=IDENTITY,
                bias=bias_col[:, m : m + 1],
                scale=1.0,
            )

        def place_class(c):
            for b in range(SAMPLES):
                row = b * SAMPLE_ROWS - c * CHUNK
                if 0 <= row < CHUNK:
                    p, j = divmod(row, RUN)
                    nc.scalar.copy(
                        out=biased[c][:, :, j, p : p + 1], in_=cls_mean[:, :, b : b + 1]
                    )

        def finish(c, half):
            tiles = slice(2 * half, 2 * half + 2)
            for j in range(2 * half, 2 * half + 2):
                back = psum.tile([P, D], F32, tag="bank")
                if c == CHUNKS - 1 and j % 2 == 0:
                    nc.tensor.matmul(
                        back[:], lhsT=ident_bf16[:], rhs=x_chunks[c][:, j, :], start=True, stop=False
                    )
                    for m in range(D_TILES):
                        nc.tensor.matmul(
                            back[:, m * P : (m + 1) * P],
                            lhsT=biased[c][:, m, j, :],
                            rhs=ident[:],
                            is_transpose=True,
                            start=False,
                            stop=m == D_TILES - 1,
                        )
                    nc.scalar.copy(out=finished[c][:, j, :], in_=back[:])
                    continue
                for m in range(D_TILES):
                    nc.tensor.transpose(
                        back[:, m * P : (m + 1) * P], biased[c][:, m, j, :], ident[:]
                    )
                nc.vector.tensor_tensor(
                    out=finished[c][:, j, :], in0=back[:], in1=x_chunks[c][:, j, :], op=ADD
                )
            if c >= 5:
                nc.sync.dma_start(
                    out=chunk_rows(out, c)[:, 2 * half * D : (2 * half + 2) * D],
                    in_=finished[c][:, tiles, :].rearrange("p j d -> p (j d)"),
                )
            elif half == 1:
                nc.sync.dma_start(
                    out=chunk_rows(out, c), in_=finished[c][:].rearrange("p j d -> p (j d)")
                )

        rest_codes = const.tile([P, P], U32, align_bytes=256)
        rest_scales = const.tile([P, P], U8, align_bytes=256)

        def quantise_rest():
            first = CHUNKS * CHUNK
            nc.vector.quantize_mx(
                out=rest_codes[:].bitcast(FP8X4),
                scales=rest_scales[:],
                in_=tokens[:, first : first + P, :].rearrange("q r v -> q (r v)"),
            )

        def multiply_rest():
            rest_prod = multiply_128(rest_codes[:], rest_scales[:])
            for m in range(D_TILES):
                nc.scalar.activation(
                    out=rest_biased[:, m, 0:REST],
                    in_=rest_prod[:, m, 0:REST],
                    func=IDENTITY,
                    bias=bias_col[:, m : m + 1],
                    scale=1.0,
                )

        def finish_rest():
            rest_back = psum.tile([P, D], F32, tag="bank")
            for m in range(D_TILES):
                nc.tensor.transpose(
                    rest_back[:, m * P : (m + 1) * P], rest_biased[:, m, :], ident[:]
                )
            rest_out = const.tile([REST, D], F32, align_bytes=256)
            nc.vector.tensor_tensor(
                out=rest_out[:], in0=rest_back[0:REST, :], in1=rest_x[:], op=ADD
            )
            nc.sync.dma_start(out=rest_rows(out), in_=rest_out[:])

        for pair in range(PAIRS):
            flip(0, pair)
            if pair == 1:
                prepare_bias()
        group_w(3)
        for pair in range(2):
            flip(1, pair)
        flip_class()
        warm_up()
        quantise(0)
        group_w(0)
        group_w(1)
        quantise_w(0)
        quantise_w(1)
        quantise_w(3)
        group_w(2)
        quantise_class()
        quantise_w(2)
        flips = {0: (1, 2, 5), 1: (2, 0, 3), 2: (2, 3, 5), 3: (3, 0, 3), 4: (3, 3, 5)}
        for c in range(CHUNKS):
            if c + 1 < CHUNKS:
                quantise(c + 1)
            quarter, first, last = flips.get(c, (0, 0, 0))
            if c == 0:
                for m in (0, 1, 3, 2):
                    multiply(c, m)
                multiply_class()
                place_class(c)
                for pair in range(first, last):
                    flip(quarter, pair)
            elif c in flips:
                for m in range(D_TILES):
                    multiply(c, m)
                place_class(c)
                for half in range(2):
                    finish(c - 1, half)
                for pair in range(first, last):
                    flip(quarter, pair)
            else:
                for m in range(D_TILES):
                    multiply(c, m)
                place_class(c)
                for half in range(2):
                    finish(c - 1, half)
            if c == CHUNKS - 3:
                quantise_rest()
            if c == CHUNKS - 2:
                multiply_rest()
            if c == CHUNKS - 1:
                finish_rest()
        for half in range(2):
            finish(CHUNKS - 1, half)
